import numpy as np
import ml_dtypes


def mxq(x, axis, fmt="e4m3"):
    dtype, down = {"e4m3": (ml_dtypes.float8_e4m3fn, 7), "e5m2": (ml_dtypes.float8_e5m2, 14)}[fmt]
    v = np.moveaxis(np.asarray(x, np.float32).astype(ml_dtypes.bfloat16).astype(np.float64), axis, -1)
    blocks = v.reshape(v.shape[:-1] + (-1, 32))
    amax = np.abs(blocks).max(-1, keepdims=True)
    byte = np.maximum(np.where(amax > 0, np.frexp(amax)[1] - 1 + 127, 0) - down, 1)
    scale = np.exp2(byte - 127.0)
    codes = (blocks / scale).astype(np.float32).astype(dtype).astype(np.float64)
    return np.moveaxis((codes * scale).reshape(v.shape), -1, axis)


WIDE = False


def mx_kscale(k):
    if not WIDE:
        return np.ones(k)
    levels = np.array([10, -10, 5, -5, 0])
    a = np.random.permutation(np.resize(levels, k // 512 * 4)).reshape(k // 512, 4)
    idx = np.arange(k)
    return np.exp2(a[idx // 512, idx % 128 // 32])


BF16 = ml_dtypes.bfloat16


def bf(x):
    return np.asarray(x, np.float32).astype(BF16)


def f64(x):
    return np.asarray(x).astype(np.float64)


E2M1 = np.array([0.0, 0.5, 1.0, 1.5, 2.0, 3.0, 4.0, 6.0, -0.0, -0.5, -1.0, -1.5, -2.0, -3.0, -4.0, -6.0])


def pack_weight(w, fmt):
    k, n = w.shape
    w = f64(bf(w)).reshape(k // 32, 32, n)
    amax = np.abs(w).max(1)
    if fmt == "e4m3":
        byte = np.frexp(amax)[1] - 1 + 127 - 7
    else:
        mant, ex = np.frexp(amax / 6.0)
        byte = np.where(mant > 0.5, ex, ex - 1) + 127
    byte = np.clip(np.where(amax > 0, byte, 1), 1, 254)
    scaled = (w * np.exp2(127.0 - byte)[:, None, :]).reshape(k, n).astype(np.float32)
    by_word = np.ascontiguousarray(scaled.reshape(k // 512, 128, 4, n).transpose(0, 1, 3, 2))
    if fmt == "e4m3":
        words = by_word.astype(ml_dtypes.float8_e4m3fn).view(np.uint8)
    else:
        c = by_word.astype(ml_dtypes.float4_e2m1fn).view(np.uint8) & 0xF
        words = c[..., 0::2] | (c[..., 1::2] << 4)
    return np.ascontiguousarray(words), np.ascontiguousarray(byte.astype(np.uint8).reshape(k // 512, 16, n))


def unpack_weight(words, scales, fmt):
    g, p, n, _ = words.shape
    if fmt == "e4m3":
        vals = np.ascontiguousarray(words).view(ml_dtypes.float8_e4m3fn).astype(np.float64)
    else:
        nib = np.empty((g, p, n, 4), np.uint8)
        nib[..., 0::2] = words & 0xF
        nib[..., 1::2] = words >> 4
        vals = E2M1[nib]
    vals = vals * np.repeat(np.exp2(scales.astype(np.float64) - 127.0), 8, axis=1)[..., None]
    return vals.transpose(0, 1, 3, 2).reshape(g * 512, n)

def pack4(w):
    words, scales = pack_weight(w, "e2m1")
    return words.reshape(words.shape[0], 128, -1), scales


def unpack4(words, scales):
    return unpack_weight(words.reshape(words.shape[0], 128, -1, 2), scales, "e2m1")


B, A, S, R, H = 512, 32, 512, 1024, 1024


def sigmoid(v):
    return 1.0 / (1.0 + np.exp(-v))


def elu(v):
    return np.where(v > 0.0, v, np.exp(np.minimum(v, 0.0)) - 1.0)


def setup_inputs():
    s = mx_kscale(H)
    h = bf(elu(np.random.standard_normal((B, H))) * s)
    prev_rnn_hidden = bf(np.random.standard_normal((B, R)))
    W_ih_words, W_ih_scales = pack4((np.random.standard_normal((3 * R, H)) / np.sqrt(H) / s[None, :]).T)
    W_hh_words, W_hh_scales = pack4((np.random.standard_normal((3 * R, R)) / np.sqrt(R)).T)
    b_ih = bf(np.random.standard_normal(3 * R) * 0.3)
    b_n = bf(np.random.standard_normal(R) * 0.3)
    return {"h": h,
            "prev_rnn_hidden": prev_rnn_hidden,
            "W_ih_words": W_ih_words,
            "W_ih_scales": W_ih_scales,
            "W_hh_words": W_hh_words,
            "W_hh_scales": W_hh_scales,
            "b_ih": b_ih,
            "b_n": b_n}


def reference(h, prev_rnn_hidden, W_ih_words, W_ih_scales, W_hh_words, W_hh_scales, b_ih, b_n):
    hp = f64(prev_rnn_hidden)
    igates = (mxq(f64(h), 1, "e4m3") @ unpack4(W_ih_words, W_ih_scales)) + f64(b_ih)
    hgates = mxq(hp, 1, "e4m3") @ unpack4(W_hh_words, W_hh_scales)
    ig_r, ig_z, ig_n = np.split(igates, 3, axis=-1)
    hg_r, hg_z, hg_n = np.split(hgates, 3, axis=-1)
    reset = sigmoid(ig_r + hg_r)
    update = sigmoid(ig_z + hg_z)
    new = np.tanh(ig_n + reset * (hg_n + f64(b_n)))
    return new + update * (hp - new)

@@ -1,0 +1,209 @@
+from contextlib import ExitStack
+
+import concourse.mybir as mybir
+from concourse.masks import make_identity
+
+F32 = mybir.dt.float32
+BF16 = mybir.dt.bfloat16
+I32 = mybir.dt.int32
+U32 = mybir.dt.uint32
+U8 = mybir.dt.uint8
+FP8X4 = mybir.dt.float8_e4m3fn_x4
+FP4X4 = mybir.dt.float4_e2m1fn_x4
+ACT = mybir.ActivationFunctionType
+ALU = mybir.AluOpType
+
+P = 128
+ROWS = 512
+ROW_TILES = ROWS // P
+K = 1024
+K_PASS = 512
+K_GROUPS = K // K_PASS
+R = 1024
+GATES = 3
+COL_TILES = R // P
+W_CHUNKS = 4
+GATE_R, GATE_Z, GATE_N = 0, 1, 2
+
+FLOPS = 2 * 2 * ROWS * K * GATES * R
+
+
+def load_scale_rows(nc, planes, scales):
+    rows = scales.rearrange("g q n -> q g n")
+    for b in range(2):
+        for r in range(4):
+            nc.sync.dma_start(
+                out=planes[32 * b + r : P : 64, :, :].bitcast(I32),
+                in_=rows[4 * b + r : 16 : 8, :, :].bitcast(I32),
+            )
+
+
+def load_weight_chunk(nc, words_sb, words, chunk):
+    for g in range(K_GROUPS):
+        nc.sync.dma_start(
+            out=words_sb[:, g, :]
+            .rearrange("p (gate c b) -> p gate c b", gate=GATES, c=W_CHUNKS)[:, :, chunk, :]
+            .bitcast(I32),
+            in_=words[g]
+            .rearrange("p (gate c b) -> p gate c b", gate=GATES, c=W_CHUNKS)[:, :, chunk, :]
+            .bitcast(I32),
+        )
+
+
+def tile_prior_pa_kernel(
+    tc, h, prev_rnn_hidden, W_ih_words, W_ih_scales, W_hh_words, W_hh_scales, b_ih, b_n, out
+):
+    nc = tc.nc
+    with ExitStack() as stack:
+        keep = stack.enter_context(tc.tile_pool(name="keep", bufs=1))
+        work = stack.enter_context(tc.tile_pool(name="work", bufs=3))
+        psum = stack.enter_context(tc.psum_pool(name="psum", bufs=8))
+        stack.enter_context(tc.manual_schedule())
+
+        zero_col = keep.tile([P, 1], F32)
+        nc.vector.memset(zero_col[:], 0.0)
+        ih_planes = keep.tile([P, K_GROUPS, GATES * R], U8, align_bytes=64)
+        hh_planes = keep.tile([P, K_GROUPS, GATES * R], U8, align_bytes=64)
+        nc.vector.memset(ih_planes[:].rearrange("p g n -> p (g n)").bitcast(I32), 0)
+        nc.vector.memset(hh_planes[:].rearrange("p g n -> p (g n)").bitcast(I32), 0)
+        bias_rows = keep.tile([P, P], BF16)
+        nc.vector.memset(bias_rows[:], 0.0)
+        half_col = keep.tile([P, 1], F32)
+        nc.scalar.activation(out=half_col[:], in_=zero_col[:], func=ACT.Sigmoid)
+        ident_f32 = keep.tile([P, P], F32)
+        make_identity(nc, ident_f32[:])
+        ident_bf16 = keep.tile([P, P], BF16)
+        make_identity(nc, ident_bf16[:])
+
+        x_dram = (h, prev_rnn_hidden)
+        x_sb = []
+        for x in range(2):
+            rows_sb = keep.tile([P, ROW_TILES, K], BF16, name="x_sb%d" % x)
+            nc.sync.dma_start(out=rows_sb[:], in_=x_dram[x].rearrange("(p m) k -> p m k", m=ROW_TILES))
+            x_sb.append(rows_sb)
+        hp_sb = x_sb[1]
+        nc.scalar.dma_start(out=bias_rows[0 : GATES * COL_TILES, :], in_=b_ih.rearrange("(c p) -> c p", p=P))
+        nc.scalar.dma_start(
+            out=bias_rows[GATES * COL_TILES : (GATES + 1) * COL_TILES, :], in_=b_n.rearrange("(c p) -> c p", p=P)
+        )
+        load_scale_rows(nc, ih_planes, W_ih_scales)
+        load_scale_rows(nc, hh_planes, W_hh_scales)
+        ih_words = keep.tile([P, K_GROUPS, 2 * GATES * R], U8, align_bytes=64)
+        hh_words = keep.tile([P, K_GROUPS, 2 * GATES * R], U8, align_bytes=64)
+        for chunk in range(W_CHUNKS):
+            load_weight_chunk(nc, ih_words, W_ih_words, chunk)
+            load_weight_chunk(nc, hh_words, W_hh_words, chunk)
+
+        x_codes = keep.tile([P, 2, K_GROUPS, ROWS], U32, align_bytes=64)
+        x_planes = keep.tile([P, 2, K_GROUPS, ROWS], U8, align_bytes=64)
+        half_rows = ROWS // 2
+        grouped = {}
+        for x in range(2):
+            words_in = x_sb[x][:].bitcast(F32)
+            for g in range(K_GROUPS):
+                quads = keep.tile([P, ROWS, 4], BF16, name="grouped%d%d" % (x, g), align_bytes=64)
+                grouped[(x, g)] = quads
+                pairs = quads[:].rearrange("p c t -> p (c t)").bitcast(F32).rearrange("p (c u) -> p c u", u=2)
+                for half in range(2):
+                    flipped = psum.tile([P, 2, half_rows], F32, tag="bank")
+                    for mm in range(ROW_TILES // 2):
+                        for u in range(2):
+                            nc.tensor.transpose(
+                                out=flipped[:, u, P * mm : P * (mm + 1)],
+                                in_=words_in[:, 2 * half + mm, 256 * g + u : 256 * (g + 1) : 2],
+                                identity=ident_f32[:],
+                            )
+                    copy = nc.vector.tensor_copy if half == 0 else nc.scalar.copy
+                    copy(
+                        out=pairs[:, half_rows * half : half_rows * (half + 1), :],
+                        in_=flipped[:].rearrange("p u c -> p c u"),
+                    )
+            for g in range(K_GROUPS):
+                nc.vector.quantize_mx(
+                    out=x_codes[:, x, g, :].bitcast(FP8X4),
+                    scales=x_planes[:, x, g, :],
+                    in_=grouped[(x, g)][:].rearrange("p c t -> p (c t)"),
+                )
+
+        bias_flipped = psum.tile([P, P], BF16, tag="bank")
+        nc.tensor.transpose(out=bias_flipped[:], in_=bias_rows[:], identity=ident_bf16[:])
+        bias_cols = keep.tile([P, (GATES + 1) * COL_TILES], F32)
+        nc.vector.tensor_copy(out=bias_cols[:], in_=bias_flipped[:, 0 : (GATES + 1) * COL_TILES])
+
+        hp_cols = keep.tile([P, COL_TILES, ROWS], BF16)
+        for pair in range(COL_TILES // 2):
+            hp_flipped = psum.tile([P, 2, ROWS], BF16, tag="bank")
+            for jj in range(2):
+                for m in range(ROW_TILES):
+                    j = 2 * pair + jj
+                    nc.tensor.transpose(
+                        out=hp_flipped[:, jj, P * m : P * (m + 1)],
+                        in_=hp_sb[:, m, P * j : P * (j + 1)],
+                        identity=ident_bf16[:],
+                    )
+            nc.scalar.copy(out=hp_cols[:, 2 * pair : 2 * pair + 2, :], in_=hp_flipped[:])
+
+        from_h = (ih_words, ih_planes, 0)
+        from_hp = (hh_words, hh_planes, 1)
+
+        def mx_group(acc, gate, j, sources):
+            col = gate * R + j * P
+            last = len(sources) * K_GROUPS - 1
+            step = 0
+            for words_sb, planes, x in sources:
+                for g in range(K_GROUPS):
+                    nc.tensor.matmul_mx(
+                        out=acc[:],
+                        lhsT=words_sb[:, g, 2 * col : 2 * (col + P)].bitcast(FP4X4),
+                        lhsT_scale=planes[:, g, col : col + P],
+                        rhs=x_codes[:, x, g, :].bitcast(FP8X4),
+                        rhs_scale=x_planes[:, x, g, :],
+                        start=(step == 0),
+                        stop=(step == last),
+                    )
+                    step += 1
+
+        def bias_of(block, j):
+            return bias_cols[:, block * COL_TILES + j : block * COL_TILES + j + 1]
+
+        out_view = out.rearrange("(p m) n -> p m n", m=ROW_TILES)
+        blended = {}
+        for j in range(COL_TILES + 1):
+            if j < COL_TILES:
+                acc_r = psum.tile([P, ROWS], F32, tag="bank")
+                mx_group(acc_r, GATE_R, j, (from_h, from_hp))
+                acc_hn = psum.tile([P, ROWS], F32, tag="bank")
+                mx_group(acc_hn, GATE_N, j, (from_hp,))
+                acc_in = psum.tile([P, ROWS], F32, tag="bank")
+                mx_group(acc_in, GATE_N, j, (from_h,))
+                acc_z = psum.tile([P, ROWS], F32, tag="bank")
+                mx_group(acc_z, GATE_Z, j, (from_h, from_hp))
+
+                reset = work.tile([P, ROWS], F32)
+                nc.scalar.activation(out=reset[:], in_=acc_r[:], func=ACT.Sigmoid, bias=bias_of(GATE_R, j))
+                gated_hn = work.tile([P, ROWS], F32)
+                nc.vector.scalar_tensor_tensor(
+                    out=gated_hn[:], in0=acc_hn[:], scalar=bias_of(GATES, j), in1=reset[:], op0=ALU.add, op1=ALU.mult
+                )
+                pre_new = work.tile([P, ROWS], F32)
+                nc.vector.tensor_tensor(out=pre_new[:], in0=gated_hn[:], in1=acc_in[:], op=ALU.add)
+                new = work.tile([P, ROWS], F32)
+                nc.scalar.activation(out=new[:], in_=pre_new[:], func=ACT.Tanh, bias=bias_of(GATE_N, j))
+                update = work.tile([P, ROWS], F32)
+                nc.scalar.activation(out=update[:], in_=acc_z[:], func=ACT.Sigmoid, bias=bias_of(GATE_Z, j))
+                diff = work.tile([P, ROWS], F32)
+                nc.vector.tensor_tensor(out=diff[:], in0=hp_cols[:, j, :], in1=new[:], op=ALU.subtract)
+                moved = work.tile([P, ROWS], F32)
+                nc.vector.tensor_tensor(out=moved[:], in0=update[:], in1=diff[:], op=ALU.mult)
+                blend = work.tile([P, ROWS], F32)
+                nc.vector.tensor_tensor(out=blend[:], in0=new[:], in1=moved[:], op=ALU.add)
+                blended[j] = blend
+            if j > 0:
+                back = psum.tile([P, ROW_TILES, P], F32, tag="bank")
+                for m in range(ROW_TILES):
+                    nc.tensor.transpose(
+                        out=back[:, m, :], in_=blended[j - 1][:, P * m : P * (m + 1)], identity=ident_f32[:]
+                    )
+                out_rows = work.tile([P, ROW_TILES, P], F32)
+                nc.scalar.copy(out=out_rows[:], in_=back[:])
+                nc.sync.dma_start(out=out_view[:, :, P * (j - 1) : P * j], in_=out_rows[:])

@@ -129,6 +129,10 @@ def tile_prior_pa_kernel(
         nc.tensor.transpose(out=bias_flipped[:], in_=bias_rows[:], identity=ident_bf16[:])
         bias_cols = keep.tile([P, (GATES + 1) * COL_TILES], F32)
         nc.vector.tensor_copy(out=bias_cols[:], in_=bias_flipped[:, 0 : (GATES + 1) * COL_TILES])
+        minus_b_z = keep.tile([P, COL_TILES], F32)
+        nc.vector.tensor_scalar_mul(
+            out=minus_b_z[:], in0=bias_cols[:, GATE_Z * COL_TILES : (GATE_Z + 1) * COL_TILES], scalar1=-1.0
+        )
 
         hp_cols = keep.tile([P, COL_TILES, ROWS], BF16)
         for pair in range(COL_TILES // 2):
@@ -186,17 +190,25 @@ def tile_prior_pa_kernel(
                     out=gated_hn[:], in0=acc_hn[:], scalar=bias_of(GATES, j), in1=reset[:], op0=ALU.add, op1=ALU.mult
                 )
                 pre_new = work.tile([P, ROWS], F32)
-                nc.vector.tensor_tensor(out=pre_new[:], in0=gated_hn[:], in1=acc_in[:], op=ALU.add)
-                new = work.tile([P, ROWS], F32)
-                nc.scalar.activation(out=new[:], in_=pre_new[:], func=ACT.Tanh, bias=bias_of(GATE_N, j))
-                update = work.tile([P, ROWS], F32)
-                nc.scalar.activation(out=update[:], in_=acc_z[:], func=ACT.Sigmoid, bias=bias_of(GATE_Z, j))
-                diff = work.tile([P, ROWS], F32)
-                nc.vector.tensor_tensor(out=diff[:], in0=hp_cols[:, j, :], in1=new[:], op=ALU.subtract)
+                nc.vector.scalar_tensor_tensor(
+                    out=pre_new[:], in0=gated_hn[:], scalar=bias_of(GATE_N, j), in1=acc_in[:], op0=ALU.add, op1=ALU.add
+                )
+                new_sig = work.tile([P, ROWS], F32)
+                nc.scalar.activation(out=new_sig[:], in_=pre_new[:], func=ACT.Sigmoid, scale=2.0)
+                hold = work.tile([P, ROWS], F32)
+                nc.scalar.activation(
+                    out=hold[:], in_=acc_z[:], func=ACT.Sigmoid, scale=-1.0, bias=minus_b_z[:, j : j + 1]
+                )
+                diff_less_1 = work.tile([P, ROWS], F32)
+                nc.vector.scalar_tensor_tensor(
+                    out=diff_less_1[:], in0=new_sig[:], scalar=-2.0, in1=hp_cols[:, j, :], op0=ALU.mult, op1=ALU.add
+                )
                 moved = work.tile([P, ROWS], F32)
-                nc.vector.tensor_tensor(out=moved[:], in0=update[:], in1=diff[:], op=ALU.mult)
+                nc.vector.scalar_tensor_tensor(
+                    out=moved[:], in0=diff_less_1[:], scalar=1.0, in1=hold[:], op0=ALU.add, op1=ALU.mult
+                )
                 blend = work.tile([P, ROWS], F32)
-                nc.vector.tensor_tensor(out=blend[:], in0=new[:], in1=moved[:], op=ALU.add)
+                nc.vector.tensor_tensor(out=blend[:], in0=hp_cols[:, j, :], in1=moved[:], op=ALU.subtract)
                 blended[j] = blend
             if j > 0:
                 back = psum.tile([P, ROW_TILES, P], F32, tag="bank")

@@ -30,12 +30,8 @@ FLOPS = 2 * 2 * ROWS * K * GATES * R
 
 def load_scale_rows(nc, planes, scales):
     rows = scales.rearrange("g q n -> q g n")
-    for b in range(2):
-        for r in range(4):
-            nc.sync.dma_start(
-                out=planes[32 * b + r : P : 64, :, :].bitcast(I32),
-                in_=rows[4 * b + r : 16 : 8, :, :].bitcast(I32),
-            )
+    for r in range(4):
+        nc.sync.dma_start(out=planes[r:P:32, :, :].bitcast(I32), in_=rows[r:16:4, :, :].bitcast(I32))
 
 
 def load_weight_chunk(nc, words_sb, words, chunk):
@@ -56,7 +52,7 @@ def tile_prior_pa_kernel(
     nc = tc.nc
     with ExitStack() as stack:
         keep = stack.enter_context(tc.tile_pool(name="keep", bufs=1))
-        work = stack.enter_context(tc.tile_pool(name="work", bufs=3))
+        work = stack.enter_context(tc.tile_pool(name="work", bufs=4))
         psum = stack.enter_context(tc.psum_pool(name="psum", bufs=8))
         stack.enter_context(tc.manual_schedule())
 
@@ -79,7 +75,10 @@ def tile_prior_pa_kernel(
         x_sb = []
         for x in range(2):
             rows_sb = keep.tile([P, ROW_TILES, K], BF16, name="x_sb%d" % x)
-            nc.sync.dma_start(out=rows_sb[:], in_=x_dram[x].rearrange("(p m) k -> p m k", m=ROW_TILES))
+            rows_dram = x_dram[x].rearrange("(p m) k -> p m k", m=ROW_TILES)
+            for g in range(K_GROUPS):
+                k_cols = slice(K_PASS * g, K_PASS * (g + 1))
+                nc.sync.dma_start(out=rows_sb[:, :, k_cols], in_=rows_dram[:, :, k_cols])
             x_sb.append(rows_sb)
         hp_sb = x_sb[1]
         nc.scalar.dma_start(out=bias_rows[0 : GATES * COL_TILES, :], in_=b_ih.rearrange("(c p) -> c p", p=P))
@@ -129,93 +128,139 @@ def tile_prior_pa_kernel(
         nc.tensor.transpose(out=bias_flipped[:], in_=bias_rows[:], identity=ident_bf16[:])
         bias_cols = keep.tile([P, (GATES + 1) * COL_TILES], F32)
         nc.vector.tensor_copy(out=bias_cols[:], in_=bias_flipped[:, 0 : (GATES + 1) * COL_TILES])
-        minus_b_z = keep.tile([P, COL_TILES], F32)
-        nc.vector.tensor_scalar_mul(
-            out=minus_b_z[:], in0=bias_cols[:, GATE_Z * COL_TILES : (GATE_Z + 1) * COL_TILES], scalar1=-1.0
-        )
-
-        hp_cols = keep.tile([P, COL_TILES, ROWS], BF16)
-        for pair in range(COL_TILES // 2):
-            hp_flipped = psum.tile([P, 2, ROWS], BF16, tag="bank")
-            for jj in range(2):
-                for m in range(ROW_TILES):
-                    j = 2 * pair + jj
-                    nc.tensor.transpose(
-                        out=hp_flipped[:, jj, P * m : P * (m + 1)],
-                        in_=hp_sb[:, m, P * j : P * (j + 1)],
-                        identity=ident_bf16[:],
-                    )
-            nc.scalar.copy(out=hp_cols[:, 2 * pair : 2 * pair + 2, :], in_=hp_flipped[:])
 
         from_h = (ih_words, ih_planes, 0)
         from_hp = (hh_words, hh_planes, 1)
 
-        def mx_group(acc, gate, j, sources):
+        def mx_group(bank, gate, j, sources):
             col = gate * R + j * P
-            last = len(sources) * K_GROUPS - 1
-            step = 0
-            for words_sb, planes, x in sources:
-                for g in range(K_GROUPS):
-                    nc.tensor.matmul_mx(
-                        out=acc[:],
-                        lhsT=words_sb[:, g, 2 * col : 2 * (col + P)].bitcast(FP4X4),
-                        lhsT_scale=planes[:, g, col : col + P],
-                        rhs=x_codes[:, x, g, :].bitcast(FP8X4),
-                        rhs_scale=x_planes[:, x, g, :],
-                        start=(step == 0),
-                        stop=(step == last),
-                    )
-                    step += 1
+            passes = [(source, g) for source in sources for g in range(K_GROUPS)]
+            for nth, ((words_sb, planes, x), g) in enumerate(passes):
+                nc.tensor.matmul_mx(
+                    out=bank[:],
+                    lhsT=words_sb[:, g, 2 * col : 2 * (col + P)].bitcast(FP4X4),
+                    lhsT_scale=planes[:, g, col : col + P],
+                    rhs=x_codes[:, x, g, :].bitcast(FP8X4),
+                    rhs_scale=x_planes[:, x, g, :],
+                    start=(nth == 0),
+                    stop=(nth == len(passes) - 1),
+                )
 
         def bias_of(block, j):
             return bias_cols[:, block * COL_TILES + j : block * COL_TILES + j + 1]
 
         out_view = out.rearrange("(p m) n -> p m n", m=ROW_TILES)
-        blended = {}
-        for j in range(COL_TILES + 1):
-            if j < COL_TILES:
-                acc_r = psum.tile([P, ROWS], F32, tag="bank")
-                mx_group(acc_r, GATE_R, j, (from_h, from_hp))
-                acc_hn = psum.tile([P, ROWS], F32, tag="bank")
-                mx_group(acc_hn, GATE_N, j, (from_hp,))
-                acc_in = psum.tile([P, ROWS], F32, tag="bank")
-                mx_group(acc_in, GATE_N, j, (from_h,))
-                acc_z = psum.tile([P, ROWS], F32, tag="bank")
-                mx_group(acc_z, GATE_Z, j, (from_h, from_hp))
+        banks = {}
+        kept = {}
 
-                reset = work.tile([P, ROWS], F32)
-                nc.scalar.activation(out=reset[:], in_=acc_r[:], func=ACT.Sigmoid, bias=bias_of(GATE_R, j))
-                gated_hn = work.tile([P, ROWS], F32)
-                nc.vector.scalar_tensor_tensor(
-                    out=gated_hn[:], in0=acc_hn[:], scalar=bias_of(GATES, j), in1=reset[:], op0=ALU.add, op1=ALU.mult
+        sums = {
+            "r": (GATE_R, (from_h, from_hp)),
+            "z": (GATE_Z, (from_h, from_hp)),
+            "in": (GATE_N, (from_h,)),
+            "hn": (GATE_N, (from_hp,)),
+        }
+
+        def mx_sum(name, j):
+            gate, sources = sums[name]
+            banks[(name, j)] = psum.tile([P, ROWS], F32, tag="bank", name="acc_" + name)
+            mx_group(banks[(name, j)], gate, j, sources)
+
+        def flip_hp(j):
+            banks[("hp", j)] = psum.tile([P, ROWS], BF16, tag="bank", name="hp_flipped")
+            for m in range(ROW_TILES):
+                nc.tensor.transpose(
+                    out=banks[("hp", j)][:, P * m : P * (m + 1)],
+                    in_=hp_sb[:, m, P * j : P * (j + 1)],
+                    identity=ident_bf16[:],
                 )
-                pre_new = work.tile([P, ROWS], F32)
-                nc.vector.scalar_tensor_tensor(
-                    out=pre_new[:], in0=gated_hn[:], scalar=bias_of(GATE_N, j), in1=acc_in[:], op0=ALU.add, op1=ALU.add
+
+        def f32_tile(name, j):
+            kept[(name, j)] = work.tile([P, ROWS], F32, name=name, tag=name)
+            return kept[(name, j)]
+
+        def reset(j):
+            nc.scalar.activation(
+                out=f32_tile("reset", j)[:], in_=banks[("r", j)][:], func=ACT.Sigmoid, bias=bias_of(GATE_R, j)
+            )
+
+        def gated_hn(j):
+            nc.vector.scalar_tensor_tensor(
+                out=f32_tile("gated_hn", j)[:],
+                in0=banks[("hn", j)][:],
+                scalar=bias_of(GATES, j),
+                in1=kept[("reset", j)][:],
+                op0=ALU.add,
+                op1=ALU.mult,
+            )
+
+        def pre_new(j):
+            nc.vector.tensor_tensor(
+                out=f32_tile("pre_new", j)[:], in0=kept[("gated_hn", j)][:], in1=banks[("in", j)][:], op=ALU.add
+            )
+
+        def new(j):
+            nc.scalar.activation(
+                out=f32_tile("new", j)[:], in_=kept[("pre_new", j)][:], func=ACT.Tanh, bias=bias_of(GATE_N, j)
+            )
+
+        def update(j):
+            nc.scalar.activation(
+                out=f32_tile("update", j)[:], in_=banks[("z", j)][:], func=ACT.Sigmoid, bias=bias_of(GATE_Z, j)
+            )
+
+        def diff(j):
+            nc.vector.tensor_tensor(
+                out=f32_tile("diff", j)[:], in0=banks[("hp", j)][:], in1=kept[("new", j)][:], op=ALU.subtract
+            )
+
+        def moved(j):
+            nc.vector.tensor_tensor(
+                out=f32_tile("moved", j)[:], in0=kept[("update", j)][:], in1=kept[("diff", j)][:], op=ALU.mult
+            )
+
+        def blend(j):
+            nc.vector.tensor_tensor(
+                out=f32_tile("blend", j)[:], in0=kept[("new", j)][:], in1=kept[("moved", j)][:], op=ALU.add
+            )
+
+        def flip_back(j):
+            banks[("back", j)] = psum.tile([P, ROW_TILES, P], F32, tag="bank", name="back")
+            for m in range(ROW_TILES):
+                nc.tensor.transpose(
+                    out=banks[("back", j)][:, m, :],
+                    in_=kept[("blend", j)][:, P * m : P * (m + 1)],
+                    identity=ident_f32[:],
                 )
-                new_sig = work.tile([P, ROWS], F32)
-                nc.scalar.activation(out=new_sig[:], in_=pre_new[:], func=ACT.Sigmoid, scale=2.0)
-                hold = work.tile([P, ROWS], F32)
-                nc.scalar.activation(
-                    out=hold[:], in_=acc_z[:], func=ACT.Sigmoid, scale=-1.0, bias=minus_b_z[:, j : j + 1]
-                )
-                diff_less_1 = work.tile([P, ROWS], F32)
-                nc.vector.scalar_tensor_tensor(
-                    out=diff_less_1[:], in0=new_sig[:], scalar=-2.0, in1=hp_cols[:, j, :], op0=ALU.mult, op1=ALU.add
-                )
-                moved = work.tile([P, ROWS], F32)
-                nc.vector.scalar_tensor_tensor(
-                    out=moved[:], in0=diff_less_1[:], scalar=1.0, in1=hold[:], op0=ALU.add, op1=ALU.mult
-                )
-                blend = work.tile([P, ROWS], F32)
-                nc.vector.tensor_tensor(out=blend[:], in0=hp_cols[:, j, :], in1=moved[:], op=ALU.subtract)
-                blended[j] = blend
-            if j > 0:
-                back = psum.tile([P, ROW_TILES, P], F32, tag="bank")
-                for m in range(ROW_TILES):
-                    nc.tensor.transpose(
-                        out=back[:, m, :], in_=blended[j - 1][:, P * m : P * (m + 1)], identity=ident_f32[:]
-                    )
-                out_rows = work.tile([P, ROW_TILES, P], F32)
-                nc.scalar.copy(out=out_rows[:], in_=back[:])
-                nc.sync.dma_start(out=out_view[:, :, P * (j - 1) : P * j], in_=out_rows[:])
+
+        def store_rows(j):
+            out_rows = work.tile([P, ROW_TILES, P], F32)
+            nc.scalar.copy(out=out_rows[:], in_=banks[("back", j)][:])
+            nc.sync.dma_start(out=out_view[:, :, P * j : P * (j + 1)], in_=out_rows[:])
+
+        for step in range(COL_TILES + 2):
+            front, middle, rear = step, step - 1, step - 2
+            has_front = front < COL_TILES
+            has_middle = 0 <= middle < COL_TILES
+            if has_front:
+                mx_sum("r", front)
+                mx_sum("hn", front)
+                mx_sum("in", front)
+            if rear >= 0:
+                flip_back(rear)
+            if has_front:
+                flip_hp(front)
+                mx_sum("z", front)
+            if has_front:
+                reset(front)
+                gated_hn(front)
+            if has_middle:
+                new(middle)
+                update(middle)
+                diff(middle)
+            if has_front:
+                pre_new(front)
+            if has_middle:
+                moved(middle)
+                blend(middle)
+            if rear >= 0:
+                store_rows(rear)

@@ -23,6 +23,7 @@ R = 1024
 GATES = 3
 COL_TILES = R // P
 W_CHUNKS = 4
+CHUNK_TILES = COL_TILES // W_CHUNKS
 GATE_R, GATE_Z, GATE_N = 0, 1, 2
 
 FLOPS = 2 * 2 * ROWS * K * GATES * R
@@ -34,12 +35,10 @@ def load_scale_rows(nc, planes, scales):
         nc.sync.dma_start(out=planes[r:P:32, :, :].bitcast(I32), in_=rows[r:16:4, :, :].bitcast(I32))
 
 
-def load_weight_chunk(nc, words_sb, words, chunk):
+def load_weight_chunk(nc, chunk_sb, words, chunk):
     for g in range(K_GROUPS):
         nc.sync.dma_start(
-            out=words_sb[:, g, :]
-            .rearrange("p (gate c b) -> p gate c b", gate=GATES, c=W_CHUNKS)[:, :, chunk, :]
-            .bitcast(I32),
+            out=chunk_sb[:, g, :, :].bitcast(I32),
             in_=words[g]
             .rearrange("p (gate c b) -> p gate c b", gate=GATES, c=W_CHUNKS)[:, :, chunk, :]
             .bitcast(I32),
@@ -72,34 +71,37 @@ def tile_prior_pa_kernel(
         make_identity(nc, ident_bf16[:])
 
         x_dram = (h, prev_rnn_hidden)
-        x_sb = []
+        x_sb = {}
         for x in range(2):
-            rows_sb = keep.tile([P, ROW_TILES, K], BF16, name="x_sb%d" % x)
-            rows_dram = x_dram[x].rearrange("(p m) k -> p m k", m=ROW_TILES)
             for g in range(K_GROUPS):
-                k_cols = slice(K_PASS * g, K_PASS * (g + 1))
-                nc.sync.dma_start(out=rows_sb[:, :, k_cols], in_=rows_dram[:, :, k_cols])
-            x_sb.append(rows_sb)
-        hp_sb = x_sb[1]
+                x_sb[(x, g)] = keep.tile([P, ROW_TILES, K_PASS], BF16, name="x_sb%d%d" % (x, g))
+                nc.sync.dma_start(
+                    out=x_sb[(x, g)][:],
+                    in_=x_dram[x].rearrange("(p m) k -> p m k", m=ROW_TILES)[:, :, K_PASS * g : K_PASS * (g + 1)],
+                )
         nc.scalar.dma_start(out=bias_rows[0 : GATES * COL_TILES, :], in_=b_ih.rearrange("(c p) -> c p", p=P))
         nc.scalar.dma_start(
             out=bias_rows[GATES * COL_TILES : (GATES + 1) * COL_TILES, :], in_=b_n.rearrange("(c p) -> c p", p=P)
         )
         load_scale_rows(nc, ih_planes, W_ih_scales)
         load_scale_rows(nc, hh_planes, W_hh_scales)
-        ih_words = keep.tile([P, K_GROUPS, 2 * GATES * R], U8, align_bytes=64)
-        hh_words = keep.tile([P, K_GROUPS, 2 * GATES * R], U8, align_bytes=64)
+        ih_words = []
+        hh_words = []
         for chunk in range(W_CHUNKS):
-            load_weight_chunk(nc, ih_words, W_ih_words, chunk)
-            load_weight_chunk(nc, hh_words, W_hh_words, chunk)
+            for chunks, words, name in ((ih_words, W_ih_words, "ih_words"), (hh_words, W_hh_words, "hh_words")):
+                chunk_sb = keep.tile(
+                    [P, K_GROUPS, GATES, 2 * P * CHUNK_TILES], U8, name="%s%d" % (name, chunk), align_bytes=64
+                )
+                load_weight_chunk(nc, chunk_sb, words, chunk)
+                chunks.append(chunk_sb)
 
         x_codes = keep.tile([P, 2, K_GROUPS, ROWS], U32, align_bytes=64)
         x_planes = keep.tile([P, 2, K_GROUPS, ROWS], U8, align_bytes=64)
         half_rows = ROWS // 2
         grouped = {}
         for x in range(2):
-            words_in = x_sb[x][:].bitcast(F32)
             for g in range(K_GROUPS):
+                words_in = x_sb[(x, g)][:].bitcast(F32)
                 quads = keep.tile([P, ROWS, 4], BF16, name="grouped%d%d" % (x, g), align_bytes=64)
                 grouped[(x, g)] = quads
                 pairs = quads[:].rearrange("p c t -> p (c t)").bitcast(F32).rearrange("p (c u) -> p c u", u=2)
@@ -109,7 +111,7 @@ def tile_prior_pa_kernel(
                         for u in range(2):
                             nc.tensor.transpose(
                                 out=flipped[:, u, P * mm : P * (mm + 1)],
-                                in_=words_in[:, 2 * half + mm, 256 * g + u : 256 * (g + 1) : 2],
+                                in_=words_in[:, 2 * half + mm, u : K_PASS // 2 : 2],
                                 identity=ident_f32[:],
                             )
                     copy = nc.vector.tensor_copy if half == 0 else nc.scalar.copy
@@ -134,11 +136,12 @@ def tile_prior_pa_kernel(
 
         def mx_group(bank, gate, j, sources):
             col = gate * R + j * P
+            in_chunk = j % CHUNK_TILES
             passes = [(source, g) for source in sources for g in range(K_GROUPS)]
-            for nth, ((words_sb, planes, x), g) in enumerate(passes):
+            for nth, ((chunks, planes, x), g) in enumerate(passes):
                 nc.tensor.matmul_mx(
                     out=bank[:],
-                    lhsT=words_sb[:, g, 2 * col : 2 * (col + P)].bitcast(FP4X4),
+                    lhsT=chunks[j // CHUNK_TILES][:, g, gate, 2 * P * in_chunk : 2 * P * (in_chunk + 1)].bitcast(FP4X4),
                     lhsT_scale=planes[:, g, col : col + P],
                     rhs=x_codes[:, x, g, :].bitcast(FP8X4),
                     rhs_scale=x_planes[:, x, g, :],
@@ -165,12 +168,14 @@ def tile_prior_pa_kernel(
             banks[(name, j)] = psum.tile([P, ROWS], F32, tag="bank", name="acc_" + name)
             mx_group(banks[(name, j)], gate, j, sources)
 
+        tiles_a_pass = K_PASS // P
+
         def flip_hp(j):
             banks[("hp", j)] = psum.tile([P, ROWS], BF16, tag="bank", name="hp_flipped")
             for m in range(ROW_TILES):
                 nc.tensor.transpose(
                     out=banks[("hp", j)][:, P * m : P * (m + 1)],
-                    in_=hp_sb[:, m, P * j : P * (j + 1)],
+                    in_=x_sb[(1, j // tiles_a_pass)][:, m, P * (j % tiles_a_pass) : P * (j % tiles_a_pass + 1)],
                     identity=ident_bf16[:],
                 )
 

@@ -22,7 +22,7 @@ K_GROUPS = K // K_PASS
 R = 1024
 GATES = 3
 COL_TILES = R // P
-W_CHUNKS = 4
+W_CHUNKS = 8
 CHUNK_TILES = COL_TILES // W_CHUNKS
 GATE_R, GATE_Z, GATE_N = 0, 1, 2
 
@@ -73,11 +73,11 @@ def tile_prior_pa_kernel(
         x_dram = (h, prev_rnn_hidden)
         x_sb = {}
         for x in range(2):
-            for g in range(K_GROUPS):
-                x_sb[(x, g)] = keep.tile([P, ROW_TILES, K_PASS], BF16, name="x_sb%d%d" % (x, g))
+            for half in range(2):
+                x_sb[(x, half)] = keep.tile([P, ROW_TILES // 2, K], BF16, name="x_sb%d%d" % (x, half))
                 nc.sync.dma_start(
-                    out=x_sb[(x, g)][:],
-                    in_=x_dram[x].rearrange("(p m) k -> p m k", m=ROW_TILES)[:, :, K_PASS * g : K_PASS * (g + 1)],
+                    out=x_sb[(x, half)][:],
+                    in_=x_dram[x].rearrange("(p m) k -> p m k", m=ROW_TILES)[:, 2 * half : 2 * half + 2, :],
                 )
         nc.scalar.dma_start(out=bias_rows[0 : GATES * COL_TILES, :], in_=b_ih.rearrange("(c p) -> c p", p=P))
         nc.scalar.dma_start(
@@ -101,20 +101,22 @@ def tile_prior_pa_kernel(
         grouped = {}
         for x in range(2):
             for g in range(K_GROUPS):
-                words_in = x_sb[(x, g)][:].bitcast(F32)
-                quads = keep.tile([P, ROWS, 4], BF16, name="grouped%d%d" % (x, g), align_bytes=64)
-                grouped[(x, g)] = quads
-                pairs = quads[:].rearrange("p c t -> p (c t)").bitcast(F32).rearrange("p (c u) -> p c u", u=2)
-                for half in range(2):
+                grouped[(x, g)] = keep.tile([P, ROWS, 4], BF16, name="grouped%d%d" % (x, g), align_bytes=64)
+            for half in range(2):
+                words_in = x_sb[(x, half)][:].bitcast(F32)
+                for g in range(K_GROUPS):
                     flipped = psum.tile([P, 2, half_rows], F32, tag="bank")
                     for mm in range(ROW_TILES // 2):
                         for u in range(2):
                             nc.tensor.transpose(
                                 out=flipped[:, u, P * mm : P * (mm + 1)],
-                                in_=words_in[:, 2 * half + mm, u : K_PASS // 2 : 2],
+                                in_=words_in[:, mm, K_PASS // 2 * g + u : K_PASS // 2 * (g + 1) : 2],
                                 identity=ident_f32[:],
                             )
-                    copy = nc.vector.tensor_copy if half == 0 else nc.scalar.copy
+                    pairs = (
+                        grouped[(x, g)][:].rearrange("p c t -> p (c t)").bitcast(F32).rearrange("p (c u) -> p c u", u=2)
+                    )
+                    copy = nc.vector.tensor_copy if g == 0 else nc.scalar.copy
                     copy(
                         out=pairs[:, half_rows * half : half_rows * (half + 1), :],
                         in_=flipped[:].rearrange("p u c -> p c u"),
@@ -168,14 +170,12 @@ def tile_prior_pa_kernel(
             banks[(name, j)] = psum.tile([P, ROWS], F32, tag="bank", name="acc_" + name)
             mx_group(banks[(name, j)], gate, j, sources)
 
-        tiles_a_pass = K_PASS // P
-
         def flip_hp(j):
             banks[("hp", j)] = psum.tile([P, ROWS], BF16, tag="bank", name="hp_flipped")
             for m in range(ROW_TILES):
                 nc.tensor.transpose(
                     out=banks[("hp", j)][:, P * m : P * (m + 1)],
-                    in_=x_sb[(1, j // tiles_a_pass)][:, m, P * (j % tiles_a_pass) : P * (j % tiles_a_pass + 1)],
+                    in_=x_sb[(1, m // 2)][:, m % 2, P * j : P * (j + 1)],
                     identity=ident_bf16[:],
                 )
 

@@ -22,7 +22,7 @@ K_GROUPS = K // K_PASS
 R = 1024
 GATES = 3
 COL_TILES = R // P
-W_CHUNKS = 8
+W_CHUNKS = 4
 CHUNK_TILES = COL_TILES // W_CHUNKS
 GATE_R, GATE_Z, GATE_N = 0, 1, 2
 
@@ -51,7 +51,7 @@ def tile_prior_pa_kernel(
     nc = tc.nc
     with ExitStack() as stack:
         keep = stack.enter_context(tc.tile_pool(name="keep", bufs=1))
-        work = stack.enter_context(tc.tile_pool(name="work", bufs=4))
+        work = stack.enter_context(tc.tile_pool(name="work", bufs=5))
         psum = stack.enter_context(tc.psum_pool(name="psum", bufs=8))
         stack.enter_context(tc.manual_schedule())
 
@@ -73,11 +73,11 @@ def tile_prior_pa_kernel(
         x_dram = (h, prev_rnn_hidden)
         x_sb = {}
         for x in range(2):
-            for half in range(2):
-                x_sb[(x, half)] = keep.tile([P, ROW_TILES // 2, K], BF16, name="x_sb%d%d" % (x, half))
+            for g in range(K_GROUPS):
+                x_sb[(x, g)] = keep.tile([P, ROW_TILES, K_PASS], BF16, name="x_sb%d%d" % (x, g))
                 nc.sync.dma_start(
-                    out=x_sb[(x, half)][:],
-                    in_=x_dram[x].rearrange("(p m) k -> p m k", m=ROW_TILES)[:, 2 * half : 2 * half + 2, :],
+                    out=x_sb[(x, g)][:],
+                    in_=x_dram[x].rearrange("(p m) k -> p m k", m=ROW_TILES)[:, :, K_PASS * g : K_PASS * (g + 1)],
                 )
         nc.scalar.dma_start(out=bias_rows[0 : GATES * COL_TILES, :], in_=b_ih.rearrange("(c p) -> c p", p=P))
         nc.scalar.dma_start(
@@ -101,22 +101,20 @@ def tile_prior_pa_kernel(
         grouped = {}
         for x in range(2):
             for g in range(K_GROUPS):
-                grouped[(x, g)] = keep.tile([P, ROWS, 4], BF16, name="grouped%d%d" % (x, g), align_bytes=64)
-            for half in range(2):
-                words_in = x_sb[(x, half)][:].bitcast(F32)
-                for g in range(K_GROUPS):
+                words_in = x_sb[(x, g)][:].bitcast(F32)
+                quads = keep.tile([P, ROWS, 4], BF16, name="grouped%d%d" % (x, g), align_bytes=64)
+                grouped[(x, g)] = quads
+                pairs = quads[:].rearrange("p c t -> p (c t)").bitcast(F32).rearrange("p (c u) -> p c u", u=2)
+                for half in range(2):
                     flipped = psum.tile([P, 2, half_rows], F32, tag="bank")
                     for mm in range(ROW_TILES // 2):
                         for u in range(2):
                             nc.tensor.transpose(
                                 out=flipped[:, u, P * mm : P * (mm + 1)],
-                                in_=words_in[:, mm, K_PASS // 2 * g + u : K_PASS // 2 * (g + 1) : 2],
+                                in_=words_in[:, 2 * half + mm, u : K_PASS // 2 : 2],
                                 identity=ident_f32[:],
                             )
-                    pairs = (
-                        grouped[(x, g)][:].rearrange("p c t -> p (c t)").bitcast(F32).rearrange("p (c u) -> p c u", u=2)
-                    )
-                    copy = nc.vector.tensor_copy if g == 0 else nc.scalar.copy
+                    copy = nc.vector.tensor_copy if half == 0 else nc.scalar.copy
                     copy(
                         out=pairs[:, half_rows * half : half_rows * (half + 1), :],
                         in_=flipped[:].rearrange("p u c -> p c u"),
@@ -170,12 +168,14 @@ def tile_prior_pa_kernel(
             banks[(name, j)] = psum.tile([P, ROWS], F32, tag="bank", name="acc_" + name)
             mx_group(banks[(name, j)], gate, j, sources)
 
+        tiles_a_pass = K_PASS // P
+
         def flip_hp(j):
             banks[("hp", j)] = psum.tile([P, ROWS], BF16, tag="bank", name="hp_flipped")
             for m in range(ROW_TILES):
                 nc.tensor.transpose(
                     out=banks[("hp", j)][:, P * m : P * (m + 1)],
-                    in_=x_sb[(1, m // 2)][:, m % 2, P * j : P * (j + 1)],
+                    in_=x_sb[(1, j // tiles_a_pass)][:, m, P * (j % tiles_a_pass) : P * (j % tiles_a_pass + 1)],
                     identity=ident_bf16[:],
                 )
 
@@ -242,8 +242,8 @@ def tile_prior_pa_kernel(
             nc.scalar.copy(out=out_rows[:], in_=banks[("back", j)][:])
             nc.sync.dma_start(out=out_view[:, :, P * j : P * (j + 1)], in_=out_rows[:])
 
-        for step in range(COL_TILES + 2):
-            front, middle, rear = step, step - 1, step - 2
+        for step in range(COL_TILES + 3):
+            front, middle, rear = step, step - 1, step - 3
             has_front = front < COL_TILES
             has_middle = 0 <= middle < COL_TILES
             if has_front:

@@ -21,34 +21,24 @@ K_PASS = 512
 K_GROUPS = K // K_PASS
 R = 1024
 GATES = 3
-COL_TILES = R // P
-W_CHUNKS = 4
-CHUNK_TILES = COL_TILES // W_CHUNKS
 GATE_R, GATE_Z, GATE_N = 0, 1, 2
+COL_TILES = R // P
+RN_CHUNKS = 4
+CHUNK_TILES = COL_TILES // RN_CHUNKS
+HALVES = 2
+HALF = R // HALVES
+HALF_TILES = HALF // P
 
 FLOPS = 2 * 2 * ROWS * K * GATES * R
-
-
-def load_scale_rows(nc, planes, scales):
-    rows = scales.rearrange("g q n -> q g n")
-    for r in range(4):
-        nc.sync.dma_start(out=planes[r:P:32, :, :].bitcast(I32), in_=rows[r:16:4, :, :].bitcast(I32))
-
-
-def load_weight_chunk(nc, chunk_sb, words, chunk):
-    for g in range(K_GROUPS):
-        nc.sync.dma_start(
-            out=chunk_sb[:, g, :, :].bitcast(I32),
-            in_=words[g]
-            .rearrange("p (gate c b) -> p gate c b", gate=GATES, c=W_CHUNKS)[:, :, chunk, :]
-            .bitcast(I32),
-        )
 
 
 def tile_prior_pa_kernel(
     tc, h, prev_rnn_hidden, W_ih_words, W_ih_scales, W_hh_words, W_hh_scales, b_ih, b_n, out
 ):
     nc = tc.nc
+    x_dram = (h, prev_rnn_hidden)
+    words_dram = (W_ih_words, W_hh_words)
+    scales_dram = (W_ih_scales, W_hh_scales)
     with ExitStack() as stack:
         keep = stack.enter_context(tc.tile_pool(name="keep", bufs=1))
         work = stack.enter_context(tc.tile_pool(name="work", bufs=5))
@@ -57,127 +47,213 @@ def tile_prior_pa_kernel(
 
         zero_col = keep.tile([P, 1], F32)
         nc.vector.memset(zero_col[:], 0.0)
-        ih_planes = keep.tile([P, K_GROUPS, GATES * R], U8, align_bytes=64)
-        hh_planes = keep.tile([P, K_GROUPS, GATES * R], U8, align_bytes=64)
-        nc.vector.memset(ih_planes[:].rearrange("p g n -> p (g n)").bitcast(I32), 0)
-        nc.vector.memset(hh_planes[:].rearrange("p g n -> p (g n)").bitcast(I32), 0)
-        bias_rows = keep.tile([P, P], BF16)
-        nc.vector.memset(bias_rows[:], 0.0)
         half_col = keep.tile([P, 1], F32)
         nc.scalar.activation(out=half_col[:], in_=zero_col[:], func=ACT.Sigmoid)
+        z_planes = []
+        planes = []
+        for w in range(2):
+            z_planes.append(keep.tile([P, K_GROUPS, R], U8, name="z_planes%d" % w, align_bytes=64))
+            nc.vector.memset(z_planes[w][:].rearrange("p g n -> p (g n)").bitcast(I32), 0)
+        bias_rows = keep.tile([P, P], BF16)
+        nc.vector.memset(bias_rows[:], 0.0)
+        z_bias_row = keep.tile([P, R], BF16)
+        nc.vector.memset(z_bias_row[:].bitcast(I32), 0)
+        for w in range(2):
+            planes.append(keep.tile([P, K_GROUPS, GATES * R], U8, name="planes%d" % w, align_bytes=64))
         ident_f32 = keep.tile([P, P], F32)
         make_identity(nc, ident_f32[:])
         ident_bf16 = keep.tile([P, P], BF16)
         make_identity(nc, ident_bf16[:])
+        ones = keep.tile([P, P], BF16)
+        nc.gpsimd.memset(ones[:], 1.0)
+        for w in range(2):
+            nc.gpsimd.memset(planes[w][:].rearrange("p g n -> p (g n)").bitcast(I32), 0)
 
-        x_dram = (h, prev_rnn_hidden)
         x_sb = {}
-        for x in range(2):
+
+        def load_x(x):
             for g in range(K_GROUPS):
                 x_sb[(x, g)] = keep.tile([P, ROW_TILES, K_PASS], BF16, name="x_sb%d%d" % (x, g))
                 nc.sync.dma_start(
                     out=x_sb[(x, g)][:],
                     in_=x_dram[x].rearrange("(p m) k -> p m k", m=ROW_TILES)[:, :, K_PASS * g : K_PASS * (g + 1)],
                 )
+
+        def load_scale_rows(tile, w, first, last):
+            rows = scales_dram[w].rearrange("g q n -> q g n")
+            for r in range(4):
+                nc.sync.dma_start(
+                    out=tile[r:P:32, :, :].bitcast(I32), in_=rows[r:16:4, :, first:last].bitcast(I32)
+                )
+
+        z_words = {}
+
+        def load_z_words(w, half):
+            z_words[(w, half)] = keep.tile([P, K_GROUPS, 2 * HALF], U8, name="z_words%d%d" % (w, half), align_bytes=64)
+            first = 2 * (GATE_Z * R + HALF * half)
+            nc.sync.dma_start(
+                out=z_words[(w, half)][:].bitcast(I32),
+                in_=words_dram[w].rearrange("g p b -> p g b")[:, :, first : first + 2 * HALF].bitcast(I32),
+            )
+
+        rn_words = {}
+
+        def load_rn_words(w, chunk):
+            tile = keep.tile([P, K_GROUPS, 2, 2 * P * CHUNK_TILES], U8, name="rn_words%d%d" % (w, chunk), align_bytes=64)
+            rn_words[(w, chunk)] = tile
+            for g in range(K_GROUPS):
+                nc.sync.dma_start(
+                    out=tile[:, g, :, :].bitcast(I32),
+                    in_=words_dram[w][g]
+                    .rearrange("p (gate c b) -> p gate c b", gate=GATES, c=RN_CHUNKS)[:, GATE_R : GATES : GATE_N, chunk, :]
+                    .bitcast(I32),
+                )
+
         nc.scalar.dma_start(out=bias_rows[0 : GATES * COL_TILES, :], in_=b_ih.rearrange("(c p) -> c p", p=P))
         nc.scalar.dma_start(
             out=bias_rows[GATES * COL_TILES : (GATES + 1) * COL_TILES, :], in_=b_n.rearrange("(c p) -> c p", p=P)
         )
-        load_scale_rows(nc, ih_planes, W_ih_scales)
-        load_scale_rows(nc, hh_planes, W_hh_scales)
-        ih_words = []
-        hh_words = []
-        for chunk in range(W_CHUNKS):
-            for chunks, words, name in ((ih_words, W_ih_words, "ih_words"), (hh_words, W_hh_words, "hh_words")):
-                chunk_sb = keep.tile(
-                    [P, K_GROUPS, GATES, 2 * P * CHUNK_TILES], U8, name="%s%d" % (name, chunk), align_bytes=64
-                )
-                load_weight_chunk(nc, chunk_sb, words, chunk)
-                chunks.append(chunk_sb)
+        nc.scalar.dma_start(
+            out=z_bias_row[0:1, :], in_=b_ih[GATE_Z * R : (GATE_Z + 1) * R].rearrange("(o n) -> o n", o=1)
+        )
+        load_x(0)
+        load_scale_rows(z_planes[0], 0, GATE_Z * R, (GATE_Z + 1) * R)
+        load_z_words(0, 0)
+        load_x(1)
+        load_scale_rows(z_planes[1], 1, GATE_Z * R, (GATE_Z + 1) * R)
+        load_z_words(1, 0)
+        for w in range(2):
+            load_scale_rows(planes[w], w, 0, GATES * R)
+            load_rn_words(w, 0)
+        for w in range(2):
+            load_z_words(w, 1)
+        for chunk in range(1, RN_CHUNKS):
+            for w in range(2):
+                load_rn_words(w, chunk)
 
-        x_codes = keep.tile([P, 2, K_GROUPS, ROWS], U32, align_bytes=64)
-        x_planes = keep.tile([P, 2, K_GROUPS, ROWS], U8, align_bytes=64)
         half_rows = ROWS // 2
         grouped = {}
-        for x in range(2):
-            for g in range(K_GROUPS):
-                words_in = x_sb[(x, g)][:].bitcast(F32)
-                quads = keep.tile([P, ROWS, 4], BF16, name="grouped%d%d" % (x, g), align_bytes=64)
-                grouped[(x, g)] = quads
-                pairs = quads[:].rearrange("p c t -> p (c t)").bitcast(F32).rearrange("p (c u) -> p c u", u=2)
-                for half in range(2):
-                    flipped = psum.tile([P, 2, half_rows], F32, tag="bank")
-                    for mm in range(ROW_TILES // 2):
-                        for u in range(2):
-                            nc.tensor.transpose(
-                                out=flipped[:, u, P * mm : P * (mm + 1)],
-                                in_=words_in[:, 2 * half + mm, u : K_PASS // 2 : 2],
-                                identity=ident_f32[:],
-                            )
-                    copy = nc.vector.tensor_copy if half == 0 else nc.scalar.copy
-                    copy(
-                        out=pairs[:, half_rows * half : half_rows * (half + 1), :],
-                        in_=flipped[:].rearrange("p u c -> p c u"),
-                    )
-            for g in range(K_GROUPS):
-                nc.vector.quantize_mx(
-                    out=x_codes[:, x, g, :].bitcast(FP8X4),
-                    scales=x_planes[:, x, g, :],
-                    in_=grouped[(x, g)][:].rearrange("p c t -> p (c t)"),
+        x_codes = {}
+        x_planes = {}
+
+        def flip_x(x, g, copies):
+            words_in = x_sb[(x, g)][:].bitcast(F32)
+            quads = keep.tile([P, ROWS, 4], BF16, name="grouped%d%d" % (x, g), align_bytes=64)
+            grouped[(x, g)] = quads
+            pairs = quads[:].rearrange("p c t -> p (c t)").bitcast(F32).rearrange("p (c u) -> p c u", u=2)
+            for half in range(2):
+                flipped = psum.tile([P, 2, half_rows], F32, tag="bank")
+                for mm in range(ROW_TILES // 2):
+                    for u in range(2):
+                        nc.tensor.transpose(
+                            out=flipped[:, u, P * mm : P * (mm + 1)],
+                            in_=words_in[:, 2 * half + mm, u : K_PASS // 2 : 2],
+                            identity=ident_f32[:],
+                        )
+                copies[half](
+                    out=pairs[:, half_rows * half : half_rows * (half + 1), :],
+                    in_=flipped[:].rearrange("p u c -> p c u"),
                 )
 
+        def quantise_x(x, g):
+            x_codes[(x, g)] = keep.tile([P, ROWS], U32, name="x_codes%d%d" % (x, g), align_bytes=64)
+            x_planes[(x, g)] = keep.tile([P, ROWS], U8, name="x_planes%d%d" % (x, g), align_bytes=64)
+            nc.vector.quantize_mx(
+                out=x_codes[(x, g)][:].bitcast(FP8X4),
+                scales=x_planes[(x, g)][:],
+                in_=grouped[(x, g)][:].rearrange("p c t -> p (c t)"),
+            )
+
+        z_banks = {}
+
+        def z_passes(unit, sources):
+            half, m = unit
+            if unit not in z_banks:
+                z_banks[unit] = psum.tile([P, HALF], F32, tag="bank", name="acc_z")
+            for w, g in sources:
+                nc.tensor.matmul_mx(
+                    out=z_banks[unit][:],
+                    lhsT=x_codes[(w, g)][:, P * m : P * (m + 1)].bitcast(FP8X4),
+                    lhsT_scale=x_planes[(w, g)][:, P * m : P * (m + 1)],
+                    rhs=z_words[(w, half)][:, g, :].bitcast(FP4X4),
+                    rhs_scale=z_planes[w][:, g, HALF * half : HALF * (half + 1)],
+                    start=((w, g) == (0, 0)),
+                    stop=((w, g) == (1, K_GROUPS - 1)),
+                )
+
+        z_bias = keep.tile([P, R], F32)
+        new_share = []
+        for half in range(HALVES):
+            new_share.append(keep.tile([P, ROW_TILES, HALF], F32, name="new_share%d" % half))
+        z_sum = {}
+
+        def z_add_bias(unit):
+            half, m = unit
+            z_sum[unit] = work.tile([P, HALF], F32, name="z_sum", tag="z_sum")
+            nc.vector.tensor_tensor(
+                out=z_sum[unit][:], in0=z_banks[unit][:], in1=z_bias[:, HALF * half : HALF * (half + 1)], op=ALU.add
+            )
+
+        def z_sigmoid(unit):
+            half, m = unit
+            nc.scalar.activation(out=new_share[half][:, m, :], in_=z_sum[unit][:], func=ACT.Sigmoid, scale=-1.0)
+
+        on_vector = nc.vector.tensor_copy
+        on_scalar = nc.scalar.copy
+        flip_x(0, 0, (on_vector, on_scalar))
+        quantise_x(0, 0)
+        flip_x(0, 1, (on_scalar, on_scalar))
+        quantise_x(0, 1)
         bias_flipped = psum.tile([P, P], BF16, tag="bank")
         nc.tensor.transpose(out=bias_flipped[:], in_=bias_rows[:], identity=ident_bf16[:])
         bias_cols = keep.tile([P, (GATES + 1) * COL_TILES], F32)
         nc.vector.tensor_copy(out=bias_cols[:], in_=bias_flipped[:, 0 : (GATES + 1) * COL_TILES])
+        for half in range(HALVES):
+            spread = psum.tile([P, HALF], F32, tag="bank")
+            nc.tensor.matmul(
+                spread[:], lhsT=ones[:], rhs=z_bias_row[:, HALF * half : HALF * (half + 1)], start=True, stop=True
+            )
+            nc.vector.tensor_copy(out=z_bias[:, HALF * half : HALF * (half + 1)], in_=spread[:])
+        first_units = [(0, m) for m in range(ROW_TILES)]
+        for unit in first_units:
+            z_passes(unit, [(0, 0)])
+        flip_x(1, 0, (on_vector, on_scalar))
+        flip_x(1, 1, (on_vector, on_scalar))
+        quantise_x(1, 0)
+        quantise_x(1, 1)
+        for unit in first_units:
+            z_passes(unit, [(0, 1)])
+        for unit in first_units:
+            z_passes(unit, [(1, 0)])
+        for unit in first_units:
+            z_passes(unit, [(1, 1)])
+        for unit in first_units:
+            z_add_bias(unit)
 
-        from_h = (ih_words, ih_planes, 0)
-        from_hp = (hh_words, hh_planes, 1)
+        banks = {}
+        kept = {}
 
-        def mx_group(bank, gate, j, sources):
+        def rn_sum(name, j, gate, weights):
+            bank = psum.tile([P, ROWS], F32, tag="bank", name="acc_" + name)
+            banks[(name, j)] = bank
+            in_chunk = 2 * P * (j % CHUNK_TILES)
             col = gate * R + j * P
-            in_chunk = j % CHUNK_TILES
-            passes = [(source, g) for source in sources for g in range(K_GROUPS)]
-            for nth, ((chunks, planes, x), g) in enumerate(passes):
+            passes = [(w, g) for w in weights for g in range(K_GROUPS)]
+            for w, g in passes:
                 nc.tensor.matmul_mx(
                     out=bank[:],
-                    lhsT=chunks[j // CHUNK_TILES][:, g, gate, 2 * P * in_chunk : 2 * P * (in_chunk + 1)].bitcast(FP4X4),
-                    lhsT_scale=planes[:, g, col : col + P],
-                    rhs=x_codes[:, x, g, :].bitcast(FP8X4),
-                    rhs_scale=x_planes[:, x, g, :],
-                    start=(nth == 0),
-                    stop=(nth == len(passes) - 1),
+                    lhsT=rn_words[(w, j // CHUNK_TILES)][:, g, gate // GATE_N, in_chunk : in_chunk + 2 * P].bitcast(FP4X4),
+                    lhsT_scale=planes[w][:, g, col : col + P],
+                    rhs=x_codes[(w, g)][:].bitcast(FP8X4),
+                    rhs_scale=x_planes[(w, g)][:],
+                    start=((w, g) == passes[0]),
+                    stop=((w, g) == passes[-1]),
                 )
 
         def bias_of(block, j):
             return bias_cols[:, block * COL_TILES + j : block * COL_TILES + j + 1]
 
         out_view = out.rearrange("(p m) n -> p m n", m=ROW_TILES)
-        banks = {}
-        kept = {}
-
-        sums = {
-            "r": (GATE_R, (from_h, from_hp)),
-            "z": (GATE_Z, (from_h, from_hp)),
-            "in": (GATE_N, (from_h,)),
-            "hn": (GATE_N, (from_hp,)),
-        }
-
-        def mx_sum(name, j):
-            gate, sources = sums[name]
-            banks[(name, j)] = psum.tile([P, ROWS], F32, tag="bank", name="acc_" + name)
-            mx_group(banks[(name, j)], gate, j, sources)
-
-        tiles_a_pass = K_PASS // P
-
-        def flip_hp(j):
-            banks[("hp", j)] = psum.tile([P, ROWS], BF16, tag="bank", name="hp_flipped")
-            for m in range(ROW_TILES):
-                nc.tensor.transpose(
-                    out=banks[("hp", j)][:, P * m : P * (m + 1)],
-                    in_=x_sb[(1, j // tiles_a_pass)][:, m, P * (j % tiles_a_pass) : P * (j % tiles_a_pass + 1)],
-                    identity=ident_bf16[:],
-                )
 
         def f32_tile(name, j):
             kept[(name, j)] = work.tile([P, ROWS], F32, name=name, tag=name)
@@ -208,64 +284,80 @@ def tile_prior_pa_kernel(
                 out=f32_tile("new", j)[:], in_=kept[("pre_new", j)][:], func=ACT.Tanh, bias=bias_of(GATE_N, j)
             )
 
-        def update(j):
-            nc.scalar.activation(
-                out=f32_tile("update", j)[:], in_=banks[("z", j)][:], func=ACT.Sigmoid, bias=bias_of(GATE_Z, j)
-            )
-
-        def diff(j):
-            nc.vector.tensor_tensor(
-                out=f32_tile("diff", j)[:], in0=banks[("hp", j)][:], in1=kept[("new", j)][:], op=ALU.subtract
-            )
-
-        def moved(j):
-            nc.vector.tensor_tensor(
-                out=f32_tile("moved", j)[:], in0=kept[("update", j)][:], in1=kept[("diff", j)][:], op=ALU.mult
-            )
-
-        def blend(j):
-            nc.vector.tensor_tensor(
-                out=f32_tile("blend", j)[:], in0=kept[("new", j)][:], in1=kept[("moved", j)][:], op=ALU.add
-            )
-
         def flip_back(j):
             banks[("back", j)] = psum.tile([P, ROW_TILES, P], F32, tag="bank", name="back")
             for m in range(ROW_TILES):
                 nc.tensor.transpose(
                     out=banks[("back", j)][:, m, :],
-                    in_=kept[("blend", j)][:, P * m : P * (m + 1)],
+                    in_=kept[("new", j)][:, P * m : P * (m + 1)],
                     identity=ident_f32[:],
                 )
 
-        def store_rows(j):
-            out_rows = work.tile([P, ROW_TILES, P], F32)
-            nc.scalar.copy(out=out_rows[:], in_=banks[("back", j)][:])
-            nc.sync.dma_start(out=out_view[:, :, P * j : P * (j + 1)], in_=out_rows[:])
+        def half_cols(j):
+            return slice(P * (j % HALF_TILES), P * (j % HALF_TILES + 1))
 
-        for step in range(COL_TILES + 3):
-            front, middle, rear = step, step - 1, step - 3
+        def row_tile(name, j):
+            kept[(name, j)] = work.tile([P, ROW_TILES, P], F32, name=name, tag=name)
+            return kept[(name, j)]
+
+        def diff(j):
+            nc.vector.tensor_tensor(
+                out=row_tile("diff", j)[:],
+                in0=banks[("back", j)][:],
+                in1=x_sb[(1, j // HALF_TILES)][:, :, half_cols(j)],
+                op=ALU.subtract,
+            )
+
+        def moved(j):
+            nc.vector.tensor_tensor(
+                out=row_tile("moved", j)[:],
+                in0=kept[("diff", j)][:],
+                in1=new_share[j // HALF_TILES][:, :, half_cols(j)],
+                op=ALU.mult,
+            )
+
+        def store_rows(j, engine):
+            engine.tensor_tensor(
+                out=row_tile("blend", j)[:],
+                in0=kept[("moved", j)][:],
+                in1=x_sb[(1, j // HALF_TILES)][:, :, half_cols(j)],
+                op=ALU.add,
+            )
+            nc.sync.dma_start(out=out_view[:, :, P * j : P * (j + 1)], in_=kept[("blend", j)][:])
+
+        rn_sum("r", 0, GATE_R, (0, 1))
+        z_sigmoid((0, 0))
+        reset(0)
+        z_sigmoid((0, 1))
+        for step in range(COL_TILES + 1):
+            front, back = step, step - 1
             has_front = front < COL_TILES
-            has_middle = 0 <= middle < COL_TILES
             if has_front:
-                mx_sum("r", front)
-                mx_sum("hn", front)
-                mx_sum("in", front)
-            if rear >= 0:
-                flip_back(rear)
+                rn_sum("hn", front, GATE_N, (1,))
+            if back >= 0:
+                flip_back(back)
             if has_front:
-                flip_hp(front)
-                mx_sum("z", front)
+                rn_sum("in", front, GATE_N, (0,))
+            if front + 1 < COL_TILES:
+                rn_sum("r", front + 1, GATE_R, (0, 1))
+            if front < ROW_TILES:
+                z_passes((1, front), [(w, g) for w in range(2) for g in range(K_GROUPS)])
             if has_front:
-                reset(front)
                 gated_hn(front)
-            if has_middle:
-                new(middle)
-                update(middle)
-                diff(middle)
+            if back >= 0:
+                diff(back)
             if has_front:
                 pre_new(front)
-            if has_middle:
-                moved(middle)
-                blend(middle)
-            if rear >= 0:
-                store_rows(rear)
+                new(front)
+            if back >= 0:
+                moved(back)
+                store_rows(back, nc.gpsimd if has_front else nc.vector)
+            if front == 0:
+                z_sigmoid((0, 2))
+            if front + 1 < COL_TILES:
+                reset(front + 1)
+            if front == 0:
+                z_sigmoid((0, 3))
+            if front < ROW_TILES:
+                z_add_bias((1, front))
+                z_sigmoid((1, front))

@@ -28,6 +28,7 @@ CHUNK_TILES = COL_TILES // RN_CHUNKS
 HALVES = 2
 HALF = R // HALVES
 HALF_TILES = HALF // P
+EARLY_UNITS = 2
 
 FLOPS = 2 * 2 * ROWS * K * GATES * R
 
@@ -109,24 +110,24 @@ def tile_prior_pa_kernel(
                     .bitcast(I32),
                 )
 
-        nc.scalar.dma_start(out=bias_rows[0 : GATES * COL_TILES, :], in_=b_ih.rearrange("(c p) -> c p", p=P))
-        nc.scalar.dma_start(
-            out=bias_rows[GATES * COL_TILES : (GATES + 1) * COL_TILES, :], in_=b_n.rearrange("(c p) -> c p", p=P)
-        )
-        nc.scalar.dma_start(
-            out=z_bias_row[0:1, :], in_=b_ih[GATE_Z * R : (GATE_Z + 1) * R].rearrange("(o n) -> o n", o=1)
-        )
         load_x(0)
         load_scale_rows(z_planes[0], 0, GATE_Z * R, (GATE_Z + 1) * R)
         load_z_words(0, 0)
         load_x(1)
+        nc.sync.dma_start(out=bias_rows[0 : GATES * COL_TILES, :], in_=b_ih.rearrange("(c p) -> c p", p=P))
+        nc.sync.dma_start(
+            out=bias_rows[GATES * COL_TILES : (GATES + 1) * COL_TILES, :], in_=b_n.rearrange("(c p) -> c p", p=P)
+        )
+        nc.sync.dma_start(
+            out=z_bias_row[0:1, :], in_=b_ih[GATE_Z * R : (GATE_Z + 1) * R].rearrange("(o n) -> o n", o=1)
+        )
         load_scale_rows(z_planes[1], 1, GATE_Z * R, (GATE_Z + 1) * R)
         load_z_words(1, 0)
         for w in range(2):
+            load_z_words(w, 1)
+        for w in range(2):
             load_scale_rows(planes[w], w, 0, GATES * R)
             load_rn_words(w, 0)
-        for w in range(2):
-            load_z_words(w, 1)
         for chunk in range(1, RN_CHUNKS):
             for w in range(2):
                 load_rn_words(w, chunk)
@@ -183,20 +184,31 @@ def tile_prior_pa_kernel(
 
         z_bias = keep.tile([P, R], F32)
         new_share = []
+        hp_share = []
+        kept_hp = []
         for half in range(HALVES):
             new_share.append(keep.tile([P, ROW_TILES, HALF], F32, name="new_share%d" % half))
+            hp_share.append(keep.tile([P, ROW_TILES, HALF], F32, name="hp_share%d" % half))
+            kept_hp.append(keep.tile([P, ROW_TILES, HALF], F32, name="kept_hp%d" % half))
         z_sum = {}
 
         def z_add_bias(unit):
             half, m = unit
-            z_sum[unit] = work.tile([P, HALF], F32, name="z_sum", tag="z_sum")
+            z_sum[unit] = keep.tile([P, HALF], F32, name="z_sum%d%d" % unit)
             nc.vector.tensor_tensor(
                 out=z_sum[unit][:], in0=z_banks[unit][:], in1=z_bias[:, HALF * half : HALF * (half + 1)], op=ALU.add
             )
 
-        def z_sigmoid(unit):
+        def share_new(unit):
             half, m = unit
             nc.scalar.activation(out=new_share[half][:, m, :], in_=z_sum[unit][:], func=ACT.Sigmoid, scale=-1.0)
+
+        def share_hp(unit):
+            half, m = unit
+            nc.scalar.activation(out=hp_share[half][:, m, :], in_=z_sum[unit][:], func=ACT.Sigmoid)
+            nc.gpsimd.tensor_tensor(
+                out=kept_hp[half][:, m, :], in0=hp_share[half][:, m, :], in1=x_sb[(1, half)][:, m, :], op=ALU.mult
+            )
 
         on_vector = nc.vector.tensor_copy
         on_scalar = nc.scalar.copy
@@ -204,6 +216,13 @@ def tile_prior_pa_kernel(
         quantise_x(0, 0)
         flip_x(0, 1, (on_scalar, on_scalar))
         quantise_x(0, 1)
+        first_units = [(0, m) for m in range(ROW_TILES)]
+        for unit in first_units:
+            z_passes(unit, [(0, 0)])
+        flip_x(1, 0, (on_vector, on_scalar))
+        flip_x(1, 1, (on_vector, on_scalar))
+        quantise_x(1, 0)
+        quantise_x(1, 1)
         bias_flipped = psum.tile([P, P], BF16, tag="bank")
         nc.tensor.transpose(out=bias_flipped[:], in_=bias_rows[:], identity=ident_bf16[:])
         bias_cols = keep.tile([P, (GATES + 1) * COL_TILES], F32)
@@ -214,19 +233,16 @@ def tile_prior_pa_kernel(
                 spread[:], lhsT=ones[:], rhs=z_bias_row[:, HALF * half : HALF * (half + 1)], start=True, stop=True
             )
             nc.vector.tensor_copy(out=z_bias[:, HALF * half : HALF * (half + 1)], in_=spread[:])
-        first_units = [(0, m) for m in range(ROW_TILES)]
-        for unit in first_units:
-            z_passes(unit, [(0, 0)])
-        flip_x(1, 0, (on_vector, on_scalar))
-        flip_x(1, 1, (on_vector, on_scalar))
-        quantise_x(1, 0)
-        quantise_x(1, 1)
         for unit in first_units:
             z_passes(unit, [(0, 1)])
-        for unit in first_units:
-            z_passes(unit, [(1, 0)])
-        for unit in first_units:
-            z_passes(unit, [(1, 1)])
+        early_units = [(1, m) for m in range(EARLY_UNITS)]
+        for unit in early_units:
+            z_passes(unit, [(0, 0), (0, 1)])
+        for g in range(K_GROUPS):
+            for unit in first_units:
+                z_passes(unit, [(1, g)])
+        for unit in early_units:
+            z_passes(unit, [(1, 0), (1, 1)])
         for unit in first_units:
             z_add_bias(unit)
 
@@ -274,90 +290,116 @@ def tile_prior_pa_kernel(
                 op1=ALU.mult,
             )
 
-        def pre_new(j):
+        def part_tile(name, j, ms):
+            kept[(name, j, ms)] = work.tile([P, len(ms), P], F32, name=name, tag=name)
+            return kept[(name, j, ms)]
+
+        def row_columns(ms):
+            return slice(P * ms.start, P * ms.stop)
+
+        def row_tiles(ms):
+            return slice(ms.start, ms.stop)
+
+        def pre_new(j, ms):
             nc.vector.tensor_tensor(
-                out=f32_tile("pre_new", j)[:], in0=kept[("gated_hn", j)][:], in1=banks[("in", j)][:], op=ALU.add
+                out=part_tile("pre_new", j, ms)[:].rearrange("p m c -> p (m c)"),
+                in0=kept[("gated_hn", j)][:, row_columns(ms)],
+                in1=banks[("in", j)][:, row_columns(ms)],
+                op=ALU.add,
             )
 
-        def new(j):
+        def new(j, ms):
             nc.scalar.activation(
-                out=f32_tile("new", j)[:], in_=kept[("pre_new", j)][:], func=ACT.Tanh, bias=bias_of(GATE_N, j)
+                out=part_tile("new", j, ms)[:],
+                in_=kept[("pre_new", j, ms)][:],
+                func=ACT.Tanh,
+                bias=bias_of(GATE_N, j),
             )
 
-        def flip_back(j):
-            banks[("back", j)] = psum.tile([P, ROW_TILES, P], F32, tag="bank", name="back")
-            for m in range(ROW_TILES):
-                nc.tensor.transpose(
-                    out=banks[("back", j)][:, m, :],
-                    in_=kept[("new", j)][:, P * m : P * (m + 1)],
-                    identity=ident_f32[:],
-                )
+        def flip_back(j, ms):
+            bank = psum.tile([P, len(ms), P], F32, tag="bank", name="back")
+            banks[("back", j, ms)] = bank
+            for i in range(len(ms)):
+                nc.tensor.transpose(out=bank[:, i, :], in_=kept[("new", j, ms)][:, i, :], identity=ident_f32[:])
 
         def half_cols(j):
             return slice(P * (j % HALF_TILES), P * (j % HALF_TILES + 1))
 
-        def row_tile(name, j):
-            kept[(name, j)] = work.tile([P, ROW_TILES, P], F32, name=name, tag=name)
-            return kept[(name, j)]
+        def z_tile(halves, j, ms):
+            return halves[j // HALF_TILES][:, row_tiles(ms), half_cols(j)]
 
-        def diff(j):
+        def moved(j, ms):
             nc.vector.tensor_tensor(
-                out=row_tile("diff", j)[:],
-                in0=banks[("back", j)][:],
-                in1=x_sb[(1, j // HALF_TILES)][:, :, half_cols(j)],
-                op=ALU.subtract,
-            )
-
-        def moved(j):
-            nc.vector.tensor_tensor(
-                out=row_tile("moved", j)[:],
-                in0=kept[("diff", j)][:],
-                in1=new_share[j // HALF_TILES][:, :, half_cols(j)],
+                out=part_tile("moved", j, ms)[:],
+                in0=banks[("back", j, ms)][:],
+                in1=z_tile(new_share, j, ms),
                 op=ALU.mult,
             )
 
-        def store_rows(j, engine):
+        def blend(j, ms, engine):
             engine.tensor_tensor(
-                out=row_tile("blend", j)[:],
-                in0=kept[("moved", j)][:],
-                in1=x_sb[(1, j // HALF_TILES)][:, :, half_cols(j)],
-                op=ALU.add,
+                out=part_tile("blend", j, ms)[:], in0=kept[("moved", j, ms)][:], in1=z_tile(kept_hp, j, ms), op=ALU.add
             )
-            nc.sync.dma_start(out=out_view[:, :, P * j : P * (j + 1)], in_=kept[("blend", j)][:])
+            nc.sync.dma_start(
+                out=out_view[:, row_tiles(ms), P * j : P * (j + 1)], in_=kept[("blend", j, ms)][:]
+            )
 
+        all_rows = range(ROW_TILES)
+        low_rows = range(ROW_TILES // 2)
+        high_rows = range(ROW_TILES // 2, ROW_TILES)
+        last = COL_TILES - 1
         rn_sum("r", 0, GATE_R, (0, 1))
-        z_sigmoid((0, 0))
+        share_new((0, 0))
+        share_new((0, 1))
         reset(0)
-        z_sigmoid((0, 1))
-        for step in range(COL_TILES + 1):
-            front, back = step, step - 1
-            has_front = front < COL_TILES
-            if has_front:
-                rn_sum("hn", front, GATE_N, (1,))
-            if back >= 0:
-                flip_back(back)
-            if has_front:
-                rn_sum("in", front, GATE_N, (0,))
-            if front + 1 < COL_TILES:
-                rn_sum("r", front + 1, GATE_R, (0, 1))
-            if front < ROW_TILES:
-                z_passes((1, front), [(w, g) for w in range(2) for g in range(K_GROUPS)])
-            if has_front:
-                gated_hn(front)
-            if back >= 0:
-                diff(back)
-            if has_front:
-                pre_new(front)
-                new(front)
-            if back >= 0:
-                moved(back)
-                store_rows(back, nc.gpsimd if has_front else nc.vector)
-            if front == 0:
-                z_sigmoid((0, 2))
-            if front + 1 < COL_TILES:
-                reset(front + 1)
-            if front == 0:
-                z_sigmoid((0, 3))
-            if front < ROW_TILES:
-                z_add_bias((1, front))
-                z_sigmoid((1, front))
+        for unit in early_units:
+            z_add_bias(unit)
+        share_new((0, 2))
+        share_new((0, 3))
+        share_hp((0, 0))
+        for j in range(COL_TILES):
+            rn_sum("hn", j, GATE_N, (1,))
+            if j == last:
+                flip_back(j - 1, all_rows)
+            rn_sum("in", j, GATE_N, (0,))
+            if j < last:
+                rn_sum("r", j + 1, GATE_R, (0, 1))
+            late_unit = (1, EARLY_UNITS + j)
+            if EARLY_UNITS + j < ROW_TILES:
+                z_passes(late_unit, [(w, g) for w in range(2) for g in range(K_GROUPS)])
+            gated_hn(j)
+            if j < last - 1:
+                reset(j + 1)
+            for ms in (all_rows,) if j < last else (low_rows, high_rows):
+                pre_new(j, ms)
+                new(j, ms)
+            if j == last - 1:
+                reset(j + 1)
+            if j == 0:
+                share_hp((0, 1))
+                share_hp((0, 2))
+            if j == 1:
+                share_hp((0, 3))
+                for unit in early_units:
+                    share_new(unit)
+            if j == 2:
+                for unit in early_units:
+                    share_hp(unit)
+            if EARLY_UNITS + j < ROW_TILES:
+                z_add_bias(late_unit)
+            if 2 <= j < 2 + ROW_TILES - EARLY_UNITS:
+                share_new((1, EARLY_UNITS + j - 2))
+                share_hp((1, EARLY_UNITS + j - 2))
+            if 0 < j < last:
+                flip_back(j - 1, all_rows)
+                moved(j - 1, all_rows)
+                blend(j - 1, all_rows, nc.gpsimd)
+            if j == last:
+                moved(j - 1, all_rows)
+                blend(j - 1, all_rows, nc.vector)
+        for ms in (low_rows, high_rows):
+            flip_back(last, ms)
+        for ms in (low_rows, high_rows):
+            moved(last, ms)
+        for ms in (low_rows, high_rows):
+            blend(last, ms, nc.vector)

@@ -137,6 +137,15 @@ def tile_prior_pa_kernel(
         x_codes = {}
         x_planes = {}
 
+        sorted_words = {}
+
+        def sort_words(x, g):
+            tile = keep.tile([P, ROW_TILES, 2, K_PASS // 4], F32, name="sorted%d%d" % (x, g))
+            sorted_words[(x, g)] = tile
+            nc.vector.tensor_copy(
+                out=tile[:], in_=x_sb[(x, g)][:].bitcast(F32).rearrange("p m (q u) -> p m u q", u=2)
+            )
+
         def flip_x(x, g, copies):
             words_in = x_sb[(x, g)][:].bitcast(F32)
             quads = keep.tile([P, ROWS, 4], BF16, name="grouped%d%d" % (x, g), align_bytes=64)
@@ -146,10 +155,13 @@ def tile_prior_pa_kernel(
                 flipped = psum.tile([P, 2, half_rows], F32, tag="bank")
                 for mm in range(ROW_TILES // 2):
                     for u in range(2):
+                        m = 2 * half + mm
+                        if (x, g) in sorted_words:
+                            words = sorted_words[(x, g)][:, m, u, :]
+                        else:
+                            words = words_in[:, m, u : K_PASS // 2 : 2]
                         nc.tensor.transpose(
-                            out=flipped[:, u, P * mm : P * (mm + 1)],
-                            in_=words_in[:, 2 * half + mm, u : K_PASS // 2 : 2],
-                            identity=ident_f32[:],
+                            out=flipped[:, u, P * mm : P * (mm + 1)], in_=words, identity=ident_f32[:]
                         )
                 copies[half](
                     out=pairs[:, half_rows * half : half_rows * (half + 1), :],
@@ -219,6 +231,8 @@ def tile_prior_pa_kernel(
         first_units = [(0, m) for m in range(ROW_TILES)]
         for unit in first_units:
             z_passes(unit, [(0, 0)])
+        for g in range(K_GROUPS):
+            sort_words(1, g)
         flip_x(1, 0, (on_vector, on_scalar))
         flip_x(1, 1, (on_vector, on_scalar))
         quantise_x(1, 0)
@@ -238,10 +252,7 @@ def tile_prior_pa_kernel(
         early_units = [(1, m) for m in range(EARLY_UNITS)]
         for unit in early_units:
             z_passes(unit, [(0, 0), (0, 1)])
-        for g in range(K_GROUPS):
-            for unit in first_units:
-                z_passes(unit, [(1, g)])
-        for unit in early_units:
+        for unit in first_units + early_units:
             z_passes(unit, [(1, 0), (1, 1)])
         for unit in first_units:
             z_add_bias(unit)
@@ -370,6 +381,8 @@ def tile_prior_pa_kernel(
             gated_hn(j)
             if j < last - 1:
                 reset(j + 1)
+            if j == last:
+                moved(j - 1, all_rows)
             for ms in (all_rows,) if j < last else (low_rows, high_rows):
                 pre_new(j, ms)
                 new(j, ms)
@@ -395,8 +408,7 @@ def tile_prior_pa_kernel(
                 moved(j - 1, all_rows)
                 blend(j - 1, all_rows, nc.gpsimd)
             if j == last:
-                moved(j - 1, all_rows)
-                blend(j - 1, all_rows, nc.vector)
+                blend(j - 1, all_rows, nc.gpsimd)
         for ms in (low_rows, high_rows):
             flip_back(last, ms)
         for ms in (low_rows, high_rows):

@@ -57,28 +57,30 @@ def tile_prior_pa_kernel(
             nc.vector.memset(z_planes[w][:].rearrange("p g n -> p (g n)").bitcast(I32), 0)
         bias_rows = keep.tile([P, P], BF16)
         nc.vector.memset(bias_rows[:], 0.0)
-        z_bias_row = keep.tile([P, R], BF16)
-        nc.vector.memset(z_bias_row[:].bitcast(I32), 0)
         for w in range(2):
             planes.append(keep.tile([P, K_GROUPS, GATES * R], U8, name="planes%d" % w, align_bytes=64))
         ident_f32 = keep.tile([P, P], F32)
         make_identity(nc, ident_f32[:])
         ident_bf16 = keep.tile([P, P], BF16)
         make_identity(nc, ident_bf16[:])
-        ones = keep.tile([P, P], BF16)
-        nc.gpsimd.memset(ones[:], 1.0)
         for w in range(2):
             nc.gpsimd.memset(planes[w][:].rearrange("p g n -> p (g n)").bitcast(I32), 0)
 
-        x_sb = {}
+        x_pieces = {}
 
-        def load_x(x):
+        def load_x(x, pieces):
+            count = ROW_TILES // pieces
             for g in range(K_GROUPS):
-                x_sb[(x, g)] = keep.tile([P, ROW_TILES, K_PASS], BF16, name="x_sb%d%d" % (x, g))
-                nc.sync.dma_start(
-                    out=x_sb[(x, g)][:],
-                    in_=x_dram[x].rearrange("(p m) k -> p m k", m=ROW_TILES)[:, :, K_PASS * g : K_PASS * (g + 1)],
-                )
+                x_pieces[(x, g)] = []
+                for i in range(pieces):
+                    tile = keep.tile([P, count, K_PASS], BF16, name="x_sb%d%d%d" % (x, g, i))
+                    x_pieces[(x, g)].append(tile)
+                    nc.sync.dma_start(
+                        out=tile[:],
+                        in_=x_dram[x].rearrange("(p m) k -> p m k", m=ROW_TILES)[
+                            :, count * i : count * (i + 1), K_PASS * g : K_PASS * (g + 1)
+                        ],
+                    )
 
         def load_scale_rows(tile, w, first, last):
             rows = scales_dram[w].rearrange("g q n -> q g n")
@@ -110,17 +112,13 @@ def tile_prior_pa_kernel(
                     .bitcast(I32),
                 )
 
-        load_x(0)
+        for first, vector in ((0, b_ih), (GATES * COL_TILES, b_n)):
+            rows = vector.rearrange("(c p) -> c p", p=P)
+            nc.scalar.dma_start(out=bias_rows[first : first + rows.shape[0], :], in_=rows)
+        load_x(0, 2)
         load_scale_rows(z_planes[0], 0, GATE_Z * R, (GATE_Z + 1) * R)
         load_z_words(0, 0)
-        load_x(1)
-        nc.sync.dma_start(out=bias_rows[0 : GATES * COL_TILES, :], in_=b_ih.rearrange("(c p) -> c p", p=P))
-        nc.sync.dma_start(
-            out=bias_rows[GATES * COL_TILES : (GATES + 1) * COL_TILES, :], in_=b_n.rearrange("(c p) -> c p", p=P)
-        )
-        nc.sync.dma_start(
-            out=z_bias_row[0:1, :], in_=b_ih[GATE_Z * R : (GATE_Z + 1) * R].rearrange("(o n) -> o n", o=1)
-        )
+        load_x(1, 1)
         load_scale_rows(z_planes[1], 1, GATE_Z * R, (GATE_Z + 1) * R)
         load_z_words(1, 0)
         for w in range(2):
@@ -143,11 +141,10 @@ def tile_prior_pa_kernel(
             tile = keep.tile([P, ROW_TILES, 2, K_PASS // 4], F32, name="sorted%d%d" % (x, g))
             sorted_words[(x, g)] = tile
             nc.vector.tensor_copy(
-                out=tile[:], in_=x_sb[(x, g)][:].bitcast(F32).rearrange("p m (q u) -> p m u q", u=2)
+                out=tile[:], in_=x_pieces[(x, g)][0][:].bitcast(F32).rearrange("p m (q u) -> p m u q", u=2)
             )
 
         def flip_x(x, g, copies):
-            words_in = x_sb[(x, g)][:].bitcast(F32)
             quads = keep.tile([P, ROWS, 4], BF16, name="grouped%d%d" % (x, g), align_bytes=64)
             grouped[(x, g)] = quads
             pairs = quads[:].rearrange("p c t -> p (c t)").bitcast(F32).rearrange("p (c u) -> p c u", u=2)
@@ -159,7 +156,7 @@ def tile_prior_pa_kernel(
                         if (x, g) in sorted_words:
                             words = sorted_words[(x, g)][:, m, u, :]
                         else:
-                            words = words_in[:, m, u : K_PASS // 2 : 2]
+                            words = x_pieces[(x, g)][half][:].bitcast(F32)[:, mm, u : K_PASS // 2 : 2]
                         nc.tensor.transpose(
                             out=flipped[:, u, P * mm : P * (mm + 1)], in_=words, identity=ident_f32[:]
                         )
@@ -219,7 +216,7 @@ def tile_prior_pa_kernel(
             half, m = unit
             nc.scalar.activation(out=hp_share[half][:, m, :], in_=z_sum[unit][:], func=ACT.Sigmoid)
             nc.gpsimd.tensor_tensor(
-                out=kept_hp[half][:, m, :], in0=hp_share[half][:, m, :], in1=x_sb[(1, half)][:, m, :], op=ALU.mult
+                out=kept_hp[half][:, m, :], in0=hp_share[half][:, m, :], in1=x_pieces[(1, half)][0][:, m, :], op=ALU.mult
             )
 
         on_vector = nc.vector.tensor_copy
@@ -228,27 +225,34 @@ def tile_prior_pa_kernel(
         quantise_x(0, 0)
         flip_x(0, 1, (on_scalar, on_scalar))
         quantise_x(0, 1)
+        bias_flipped = psum.tile([P, P], BF16, tag="bank")
+        nc.tensor.transpose(out=bias_flipped[:], in_=bias_rows[:], identity=ident_bf16[:])
+        spread = []
+        for half in range(HALVES):
+            spread.append(psum.tile([P, HALF_TILES, P], F32, tag="bank", name="spread"))
+            for i in range(HALF_TILES):
+                row = GATE_Z * COL_TILES + HALF_TILES * half + i
+                nc.tensor.matmul(
+                    spread[half][:, i, :],
+                    lhsT=ident_bf16[:, row : row + 1].to_broadcast([P, P]),
+                    rhs=bias_rows[:],
+                    start=True,
+                    stop=True,
+                )
         first_units = [(0, m) for m in range(ROW_TILES)]
-        for unit in first_units:
-            z_passes(unit, [(0, 0)])
+        for g in range(K_GROUPS):
+            for unit in first_units:
+                z_passes(unit, [(0, g)])
+        bias_cols = keep.tile([P, (GATES + 1) * COL_TILES], F32)
+        nc.scalar.copy(out=bias_cols[:], in_=bias_flipped[:, 0 : (GATES + 1) * COL_TILES])
+        for half in range(HALVES):
+            nc.scalar.copy(out=z_bias[:, HALF * half : HALF * (half + 1)], in_=spread[half][:].rearrange("p i c -> p (i c)"))
         for g in range(K_GROUPS):
             sort_words(1, g)
         flip_x(1, 0, (on_vector, on_scalar))
         flip_x(1, 1, (on_vector, on_scalar))
         quantise_x(1, 0)
         quantise_x(1, 1)
-        bias_flipped = psum.tile([P, P], BF16, tag="bank")
-        nc.tensor.transpose(out=bias_flipped[:], in_=bias_rows[:], identity=ident_bf16[:])
-        bias_cols = keep.tile([P, (GATES + 1) * COL_TILES], F32)
-        nc.vector.tensor_copy(out=bias_cols[:], in_=bias_flipped[:, 0 : (GATES + 1) * COL_TILES])
-        for half in range(HALVES):
-            spread = psum.tile([P, HALF], F32, tag="bank")
-            nc.tensor.matmul(
-                spread[:], lhsT=ones[:], rhs=z_bias_row[:, HALF * half : HALF * (half + 1)], start=True, stop=True
-            )
-            nc.vector.tensor_copy(out=z_bias[:, HALF * half : HALF * (half + 1)], in_=spread[:])
-        for unit in first_units:
-            z_passes(unit, [(0, 1)])
         early_units = [(1, m) for m in range(EARLY_UNITS)]
         for unit in early_units:
             z_passes(unit, [(0, 0), (0, 1)])
@@ -368,10 +372,9 @@ def tile_prior_pa_kernel(
         share_new((0, 2))
         share_new((0, 3))
         share_hp((0, 0))
+        flipped_tiles = 0
         for j in range(COL_TILES):
             rn_sum("hn", j, GATE_N, (1,))
-            if j == last:
-                flip_back(j - 1, all_rows)
             rn_sum("in", j, GATE_N, (0,))
             if j < last:
                 rn_sum("r", j + 1, GATE_R, (0, 1))
@@ -379,15 +382,11 @@ def tile_prior_pa_kernel(
             if EARLY_UNITS + j < ROW_TILES:
                 z_passes(late_unit, [(w, g) for w in range(2) for g in range(K_GROUPS)])
             gated_hn(j)
-            if j < last - 1:
+            if j < last:
                 reset(j + 1)
-            if j == last:
-                moved(j - 1, all_rows)
             for ms in (all_rows,) if j < last else (low_rows, high_rows):
                 pre_new(j, ms)
                 new(j, ms)
-            if j == last - 1:
-                reset(j + 1)
             if j == 0:
                 share_hp((0, 1))
                 share_hp((0, 2))
@@ -403,12 +402,13 @@ def tile_prior_pa_kernel(
             if 2 <= j < 2 + ROW_TILES - EARLY_UNITS:
                 share_new((1, EARLY_UNITS + j - 2))
                 share_hp((1, EARLY_UNITS + j - 2))
-            if 0 < j < last:
-                flip_back(j - 1, all_rows)
-                moved(j - 1, all_rows)
-                blend(j - 1, all_rows, nc.gpsimd)
-            if j == last:
-                blend(j - 1, all_rows, nc.gpsimd)
+            if j % 2 == 1 or j == last - 1:
+                for done in range(flipped_tiles, j):
+                    flip_back(done, all_rows)
+                for done in range(flipped_tiles, j):
+                    moved(done, all_rows)
+                    blend(done, all_rows, nc.gpsimd)
+                flipped_tiles = j
         for ms in (low_rows, high_rows):
             flip_back(last, ms)
         for ms in (low_rows, high_rows):

@@ -23,12 +23,10 @@ R = 1024
 GATES = 3
 GATE_R, GATE_Z, GATE_N = 0, 1, 2
 COL_TILES = R // P
-RN_CHUNKS = 4
-CHUNK_TILES = COL_TILES // RN_CHUNKS
+RN_RANGES = ((0, 2), (2, COL_TILES - 2))
 HALVES = 2
 HALF = R // HALVES
 HALF_TILES = HALF // P
-EARLY_UNITS = 2
 
 FLOPS = 2 * 2 * ROWS * K * GATES * R
 
@@ -66,21 +64,17 @@ def tile_prior_pa_kernel(
         for w in range(2):
             nc.gpsimd.memset(planes[w][:].rearrange("p g n -> p (g n)").bitcast(I32), 0)
 
-        x_pieces = {}
+        x_rows = ([], [])
 
         def load_x(x, pieces):
-            count = ROW_TILES // pieces
-            for g in range(K_GROUPS):
-                x_pieces[(x, g)] = []
-                for i in range(pieces):
-                    tile = keep.tile([P, count, K_PASS], BF16, name="x_sb%d%d%d" % (x, g, i))
-                    x_pieces[(x, g)].append(tile)
-                    nc.sync.dma_start(
-                        out=tile[:],
-                        in_=x_dram[x].rearrange("(p m) k -> p m k", m=ROW_TILES)[
-                            :, count * i : count * (i + 1), K_PASS * g : K_PASS * (g + 1)
-                        ],
-                    )
+            first = 0
+            for i, count in enumerate(pieces):
+                tile = keep.tile([P, count, K], BF16, name="x_sb%d%d" % (x, i))
+                nc.sync.dma_start(
+                    out=tile[:], in_=x_dram[x].rearrange("(p m) k -> p m k", m=ROW_TILES)[:, first : first + count, :]
+                )
+                x_rows[x].extend([tile[:, m, :] for m in range(count)])
+                first += count
 
         def load_scale_rows(tile, w, first, last):
             rows = scales_dram[w].rearrange("g q n -> q g n")
@@ -89,90 +83,96 @@ def tile_prior_pa_kernel(
                     out=tile[r:P:32, :, :].bitcast(I32), in_=rows[r:16:4, :, first:last].bitcast(I32)
                 )
 
-        z_words = {}
+        z_words = []
 
-        def load_z_words(w, half):
-            z_words[(w, half)] = keep.tile([P, K_GROUPS, 2 * HALF], U8, name="z_words%d%d" % (w, half), align_bytes=64)
-            first = 2 * (GATE_Z * R + HALF * half)
+        def load_z_words(w):
+            z_words.append(keep.tile([P, K_GROUPS, 2 * R], U8, name="z_words%d" % w, align_bytes=64))
             nc.sync.dma_start(
-                out=z_words[(w, half)][:].bitcast(I32),
-                in_=words_dram[w].rearrange("g p b -> p g b")[:, :, first : first + 2 * HALF].bitcast(I32),
+                out=z_words[w][:].bitcast(I32),
+                in_=words_dram[w].rearrange("g p b -> p g b")[:, :, 2 * GATE_Z * R : 2 * (GATE_Z + 1) * R].bitcast(I32),
             )
 
         rn_words = {}
 
-        def load_rn_words(w, chunk):
-            tile = keep.tile([P, K_GROUPS, 2, 2 * P * CHUNK_TILES], U8, name="rn_words%d%d" % (w, chunk), align_bytes=64)
-            rn_words[(w, chunk)] = tile
+        def load_rn_words(w, part):
+            first, count = RN_RANGES[part]
+            tile = keep.tile([P, K_GROUPS, 2, 2 * P * count], U8, name="rn_words%d%d" % (w, part), align_bytes=64)
+            rn_words[(w, part)] = tile
             for g in range(K_GROUPS):
                 nc.sync.dma_start(
                     out=tile[:, g, :, :].bitcast(I32),
                     in_=words_dram[w][g]
-                    .rearrange("p (gate c b) -> p gate c b", gate=GATES, c=RN_CHUNKS)[:, GATE_R : GATES : GATE_N, chunk, :]
+                    .rearrange("p (gate b) -> p gate b", gate=GATES)[
+                        :, GATE_R : GATES : GATE_N, 2 * P * first : 2 * P * (first + count)
+                    ]
                     .bitcast(I32),
                 )
 
         for first, vector in ((0, b_ih), (GATES * COL_TILES, b_n)):
             rows = vector.rearrange("(c p) -> c p", p=P)
             nc.scalar.dma_start(out=bias_rows[first : first + rows.shape[0], :], in_=rows)
-        load_x(0, 2)
+        load_x(0, (1, 1, 2))
         load_scale_rows(z_planes[0], 0, GATE_Z * R, (GATE_Z + 1) * R)
-        load_z_words(0, 0)
-        load_x(1, 1)
+        load_z_words(0)
+        load_x(1, (2, 2))
         load_scale_rows(z_planes[1], 1, GATE_Z * R, (GATE_Z + 1) * R)
-        load_z_words(1, 0)
-        for w in range(2):
-            load_z_words(w, 1)
+        load_z_words(1)
         for w in range(2):
             load_scale_rows(planes[w], w, 0, GATES * R)
             load_rn_words(w, 0)
-        for chunk in range(1, RN_CHUNKS):
-            for w in range(2):
-                load_rn_words(w, chunk)
+        for w in range(2):
+            load_rn_words(w, 1)
 
         half_rows = ROWS // 2
+        half_tiles = ROW_TILES // 2
         grouped = {}
         x_codes = {}
         x_planes = {}
-
+        for x in range(2):
+            for g in range(K_GROUPS):
+                grouped[(x, g)] = keep.tile([P, ROWS, 4], BF16, name="grouped%d%d" % (x, g), align_bytes=64)
+                x_codes[(x, g)] = keep.tile([P, ROWS], U32, name="x_codes%d%d" % (x, g), align_bytes=64)
+                x_planes[(x, g)] = keep.tile([P, ROWS], U8, name="x_planes%d%d" % (x, g), align_bytes=64)
         sorted_words = {}
 
-        def sort_words(x, g):
-            tile = keep.tile([P, ROW_TILES, 2, K_PASS // 4], F32, name="sorted%d%d" % (x, g))
-            sorted_words[(x, g)] = tile
-            nc.vector.tensor_copy(
-                out=tile[:], in_=x_pieces[(x, g)][0][:].bitcast(F32).rearrange("p m (q u) -> p m u q", u=2)
-            )
-
-        def flip_x(x, g, copies):
-            quads = keep.tile([P, ROWS, 4], BF16, name="grouped%d%d" % (x, g), align_bytes=64)
-            grouped[(x, g)] = quads
-            pairs = quads[:].rearrange("p c t -> p (c t)").bitcast(F32).rearrange("p (c u) -> p c u", u=2)
-            for half in range(2):
-                flipped = psum.tile([P, 2, half_rows], F32, tag="bank")
-                for mm in range(ROW_TILES // 2):
-                    for u in range(2):
-                        m = 2 * half + mm
-                        if (x, g) in sorted_words:
-                            words = sorted_words[(x, g)][:, m, u, :]
-                        else:
-                            words = x_pieces[(x, g)][half][:].bitcast(F32)[:, mm, u : K_PASS // 2 : 2]
-                        nc.tensor.transpose(
-                            out=flipped[:, u, P * mm : P * (mm + 1)], in_=words, identity=ident_f32[:]
-                        )
-                copies[half](
-                    out=pairs[:, half_rows * half : half_rows * (half + 1), :],
-                    in_=flipped[:].rearrange("p u c -> p c u"),
+        def sort_words(rows):
+            sorted_words[rows] = keep.tile([P, half_tiles, 2, K // 4], F32, name="sorted%d" % rows)
+            for mm in range(half_tiles):
+                nc.vector.tensor_copy(
+                    out=sorted_words[rows][:, mm, :, :],
+                    in_=x_rows[1][half_tiles * rows + mm].bitcast(F32).rearrange("p (q u) -> p u q", u=2),
                 )
 
-        def quantise_x(x, g):
-            x_codes[(x, g)] = keep.tile([P, ROWS], U32, name="x_codes%d%d" % (x, g), align_bytes=64)
-            x_planes[(x, g)] = keep.tile([P, ROWS], U8, name="x_planes%d%d" % (x, g), align_bytes=64)
-            nc.vector.quantize_mx(
-                out=x_codes[(x, g)][:].bitcast(FP8X4),
-                scales=x_planes[(x, g)][:],
-                in_=grouped[(x, g)][:].rearrange("p c t -> p (c t)"),
-            )
+        def words_of(x, rows, mm, g, u):
+            if x == 1:
+                return sorted_words[rows][:, mm, u, P * g : P * (g + 1)]
+            return x_rows[0][half_tiles * rows + mm].bitcast(F32)[:, K_PASS // 2 * g + u : K_PASS // 2 * (g + 1) : 2]
+
+        def flip_x(x, rows, copies):
+            flipped = [psum.tile([P, 2, half_rows], F32, tag="bank", name="flipped") for g in range(K_GROUPS)]
+            for mm in range(half_tiles):
+                for g in range(K_GROUPS):
+                    for u in range(2):
+                        nc.tensor.transpose(
+                            out=flipped[g][:, u, P * mm : P * (mm + 1)],
+                            in_=words_of(x, rows, mm, g, u),
+                            identity=ident_f32[:],
+                        )
+            for g in range(K_GROUPS):
+                pairs = grouped[(x, g)][:].rearrange("p c t -> p (c t)").bitcast(F32).rearrange("p (c u) -> p c u", u=2)
+                copies[g](
+                    out=pairs[:, half_rows * rows : half_rows * (rows + 1), :],
+                    in_=flipped[g][:].rearrange("p u c -> p c u"),
+                )
+
+        def quantise_x(x, rows):
+            columns = slice(half_rows * rows, half_rows * (rows + 1))
+            for g in range(K_GROUPS):
+                nc.vector.quantize_mx(
+                    out=x_codes[(x, g)][:, columns].bitcast(FP8X4),
+                    scales=x_planes[(x, g)][:, columns],
+                    in_=grouped[(x, g)][:, columns, :].rearrange("p c t -> p (c t)"),
+                )
 
         z_banks = {}
 
@@ -185,7 +185,7 @@ def tile_prior_pa_kernel(
                     out=z_banks[unit][:],
                     lhsT=x_codes[(w, g)][:, P * m : P * (m + 1)].bitcast(FP8X4),
                     lhsT_scale=x_planes[(w, g)][:, P * m : P * (m + 1)],
-                    rhs=z_words[(w, half)][:, g, :].bitcast(FP4X4),
+                    rhs=z_words[w][:, g, 2 * HALF * half : 2 * HALF * (half + 1)].bitcast(FP4X4),
                     rhs_scale=z_planes[w][:, g, HALF * half : HALF * (half + 1)],
                     start=((w, g) == (0, 0)),
                     stop=((w, g) == (1, K_GROUPS - 1)),
@@ -216,14 +216,14 @@ def tile_prior_pa_kernel(
             half, m = unit
             nc.scalar.activation(out=hp_share[half][:, m, :], in_=z_sum[unit][:], func=ACT.Sigmoid)
             nc.gpsimd.tensor_tensor(
-                out=kept_hp[half][:, m, :], in0=hp_share[half][:, m, :], in1=x_pieces[(1, half)][0][:, m, :], op=ALU.mult
+                out=kept_hp[half][:, m, :], in0=hp_share[half][:, m, :], in1=x_rows[1][m][:, HALF * half : HALF * (half + 1)], op=ALU.mult
             )
 
         on_vector = nc.vector.tensor_copy
         on_scalar = nc.scalar.copy
         flip_x(0, 0, (on_vector, on_scalar))
         quantise_x(0, 0)
-        flip_x(0, 1, (on_scalar, on_scalar))
+        flip_x(0, 1, (on_scalar, on_vector))
         quantise_x(0, 1)
         bias_flipped = psum.tile([P, P], BF16, tag="bank")
         nc.tensor.transpose(out=bias_flipped[:], in_=bias_rows[:], identity=ident_bf16[:])
@@ -239,26 +239,29 @@ def tile_prior_pa_kernel(
                     start=True,
                     stop=True,
                 )
+        on_h = [(0, g) for g in range(K_GROUPS)]
+        on_hp = [(1, g) for g in range(K_GROUPS)]
         first_units = [(0, m) for m in range(ROW_TILES)]
-        for g in range(K_GROUPS):
-            for unit in first_units:
-                z_passes(unit, [(0, g)])
+        second_units = [(1, m) for m in range(ROW_TILES)]
+        for unit in first_units:
+            z_passes(unit, on_h)
         bias_cols = keep.tile([P, (GATES + 1) * COL_TILES], F32)
         nc.scalar.copy(out=bias_cols[:], in_=bias_flipped[:, 0 : (GATES + 1) * COL_TILES])
         for half in range(HALVES):
             nc.scalar.copy(out=z_bias[:, HALF * half : HALF * (half + 1)], in_=spread[half][:].rearrange("p i c -> p (i c)"))
-        for g in range(K_GROUPS):
-            sort_words(1, g)
-        flip_x(1, 0, (on_vector, on_scalar))
-        flip_x(1, 1, (on_vector, on_scalar))
-        quantise_x(1, 0)
-        quantise_x(1, 1)
-        early_units = [(1, m) for m in range(EARLY_UNITS)]
-        for unit in early_units:
-            z_passes(unit, [(0, 0), (0, 1)])
-        for unit in first_units + early_units:
-            z_passes(unit, [(1, 0), (1, 1)])
-        for unit in first_units:
+        for rows in range(2):
+            sort_words(rows)
+        for rows in range(2):
+            flip_x(1, rows, (on_vector, on_scalar))
+            quantise_x(1, rows)
+        waiting_units = second_units[:2]
+        for unit in waiting_units:
+            z_passes(unit, on_h)
+        for unit in first_units + waiting_units:
+            z_passes(unit, on_hp)
+        for unit in second_units[2:]:
+            z_passes(unit, on_h + on_hp)
+        for unit in first_units + second_units:
             z_add_bias(unit)
 
         banks = {}
@@ -267,13 +270,14 @@ def tile_prior_pa_kernel(
         def rn_sum(name, j, gate, weights):
             bank = psum.tile([P, ROWS], F32, tag="bank", name="acc_" + name)
             banks[(name, j)] = bank
-            in_chunk = 2 * P * (j % CHUNK_TILES)
+            part = 0 if j < RN_RANGES[1][0] else 1
+            byte = 2 * P * (j - RN_RANGES[part][0])
             col = gate * R + j * P
             passes = [(w, g) for w in weights for g in range(K_GROUPS)]
             for w, g in passes:
                 nc.tensor.matmul_mx(
                     out=bank[:],
-                    lhsT=rn_words[(w, j // CHUNK_TILES)][:, g, gate // GATE_N, in_chunk : in_chunk + 2 * P].bitcast(FP4X4),
+                    lhsT=rn_words[(w, part)][:, g, gate // GATE_N, byte : byte + 2 * P].bitcast(FP4X4),
                     lhsT_scale=planes[w][:, g, col : col + P],
                     rhs=x_codes[(w, g)][:].bitcast(FP8X4),
                     rhs_scale=x_planes[(w, g)][:],
@@ -364,44 +368,28 @@ def tile_prior_pa_kernel(
         high_rows = range(ROW_TILES // 2, ROW_TILES)
         last = COL_TILES - 1
         rn_sum("r", 0, GATE_R, (0, 1))
-        share_new((0, 0))
-        share_new((0, 1))
+        for unit in first_units:
+            share_new(unit)
+        for unit in first_units[:2]:
+            share_hp(unit)
         reset(0)
-        for unit in early_units:
-            z_add_bias(unit)
-        share_new((0, 2))
-        share_new((0, 3))
-        share_hp((0, 0))
+        for unit in first_units[2:]:
+            share_hp(unit)
         flipped_tiles = 0
         for j in range(COL_TILES):
             rn_sum("hn", j, GATE_N, (1,))
             rn_sum("in", j, GATE_N, (0,))
             if j < last:
                 rn_sum("r", j + 1, GATE_R, (0, 1))
-            late_unit = (1, EARLY_UNITS + j)
-            if EARLY_UNITS + j < ROW_TILES:
-                z_passes(late_unit, [(w, g) for w in range(2) for g in range(K_GROUPS)])
             gated_hn(j)
             if j < last:
                 reset(j + 1)
             for ms in (all_rows,) if j < last else (low_rows, high_rows):
                 pre_new(j, ms)
                 new(j, ms)
-            if j == 0:
-                share_hp((0, 1))
-                share_hp((0, 2))
-            if j == 1:
-                share_hp((0, 3))
-                for unit in early_units:
-                    share_new(unit)
-            if j == 2:
-                for unit in early_units:
-                    share_hp(unit)
-            if EARLY_UNITS + j < ROW_TILES:
-                z_add_bias(late_unit)
-            if 2 <= j < 2 + ROW_TILES - EARLY_UNITS:
-                share_new((1, EARLY_UNITS + j - 2))
-                share_hp((1, EARLY_UNITS + j - 2))
+            if j < HALF_TILES:
+                for unit in second_units[2 * (j % 2) : 2 * (j % 2) + 2]:
+                    (share_new, share_hp)[j // 2](unit)
             if j % 2 == 1 or j == last - 1:
                 for done in range(flipped_tiles, j):
                     flip_back(done, all_rows)

@@ -24,6 +24,7 @@ GATES = 3
 GATE_R, GATE_Z, GATE_N = 0, 1, 2
 COL_TILES = R // P
 RN_RANGES = ((0, 2), (2, COL_TILES - 2))
+FLIP_STEPS = (2, 5, 6, 7)
 HALVES = 2
 HALF = R // HALVES
 HALF_TILES = HALF // P
@@ -83,14 +84,15 @@ def tile_prior_pa_kernel(
                     out=tile[r:P:32, :, :].bitcast(I32), in_=rows[r:16:4, :, first:last].bitcast(I32)
                 )
 
-        z_words = []
+        z_words = {}
 
         def load_z_words(w):
-            z_words.append(keep.tile([P, K_GROUPS, 2 * R], U8, name="z_words%d" % w, align_bytes=64))
-            nc.sync.dma_start(
-                out=z_words[w][:].bitcast(I32),
-                in_=words_dram[w].rearrange("g p b -> p g b")[:, :, 2 * GATE_Z * R : 2 * (GATE_Z + 1) * R].bitcast(I32),
-            )
+            for g in range(K_GROUPS):
+                z_words[(w, g)] = keep.tile([P, 2 * R], U8, name="z_words%d%d" % (w, g), align_bytes=64)
+                nc.sync.dma_start(
+                    out=z_words[(w, g)][:].bitcast(I32),
+                    in_=words_dram[w][g][:, 2 * GATE_Z * R : 2 * (GATE_Z + 1) * R].bitcast(I32),
+                )
 
         rn_words = {}
 
@@ -108,11 +110,11 @@ def tile_prior_pa_kernel(
                     .bitcast(I32),
                 )
 
+        load_x(0, (1, 1, 2))
+        load_scale_rows(z_planes[0], 0, GATE_Z * R, (GATE_Z + 1) * R)
         for first, vector in ((0, b_ih), (GATES * COL_TILES, b_n)):
             rows = vector.rearrange("(c p) -> c p", p=P)
             nc.scalar.dma_start(out=bias_rows[first : first + rows.shape[0], :], in_=rows)
-        load_x(0, (1, 1, 2))
-        load_scale_rows(z_planes[0], 0, GATE_Z * R, (GATE_Z + 1) * R)
         load_z_words(0)
         load_x(1, (2, 2))
         load_scale_rows(z_planes[1], 1, GATE_Z * R, (GATE_Z + 1) * R)
@@ -185,7 +187,7 @@ def tile_prior_pa_kernel(
                     out=z_banks[unit][:],
                     lhsT=x_codes[(w, g)][:, P * m : P * (m + 1)].bitcast(FP8X4),
                     lhsT_scale=x_planes[(w, g)][:, P * m : P * (m + 1)],
-                    rhs=z_words[w][:, g, 2 * HALF * half : 2 * HALF * (half + 1)].bitcast(FP4X4),
+                    rhs=z_words[(w, g)][:, 2 * HALF * half : 2 * HALF * (half + 1)].bitcast(FP4X4),
                     rhs_scale=z_planes[w][:, g, HALF * half : HALF * (half + 1)],
                     start=((w, g) == (0, 0)),
                     stop=((w, g) == (1, K_GROUPS - 1)),
@@ -243,8 +245,10 @@ def tile_prior_pa_kernel(
         on_hp = [(1, g) for g in range(K_GROUPS)]
         first_units = [(0, m) for m in range(ROW_TILES)]
         second_units = [(1, m) for m in range(ROW_TILES)]
-        for unit in first_units:
-            z_passes(unit, on_h)
+        for units in (first_units[:2], first_units[2:]):
+            for source in on_h:
+                for unit in units:
+                    z_passes(unit, [source])
         bias_cols = keep.tile([P, (GATES + 1) * COL_TILES], F32)
         nc.scalar.copy(out=bias_cols[:], in_=bias_flipped[:, 0 : (GATES + 1) * COL_TILES])
         for half in range(HALVES):
@@ -299,16 +303,6 @@ def tile_prior_pa_kernel(
                 out=f32_tile("reset", j)[:], in_=banks[("r", j)][:], func=ACT.Sigmoid, bias=bias_of(GATE_R, j)
             )
 
-        def gated_hn(j):
-            nc.vector.scalar_tensor_tensor(
-                out=f32_tile("gated_hn", j)[:],
-                in0=banks[("hn", j)][:],
-                scalar=bias_of(GATES, j),
-                in1=kept[("reset", j)][:],
-                op0=ALU.add,
-                op1=ALU.mult,
-            )
-
         def part_tile(name, j, ms):
             kept[(name, j, ms)] = work.tile([P, len(ms), P], F32, name=name, tag=name)
             return kept[(name, j, ms)]
@@ -319,10 +313,20 @@ def tile_prior_pa_kernel(
         def row_tiles(ms):
             return slice(ms.start, ms.stop)
 
+        def gated_hn(j, ms):
+            nc.vector.scalar_tensor_tensor(
+                out=part_tile("gated_hn", j, ms)[:].rearrange("p m c -> p (m c)"),
+                in0=banks[("hn", j)][:, row_columns(ms)],
+                scalar=bias_of(GATES, j),
+                in1=kept[("reset", j)][:, row_columns(ms)],
+                op0=ALU.add,
+                op1=ALU.mult,
+            )
+
         def pre_new(j, ms):
             nc.vector.tensor_tensor(
                 out=part_tile("pre_new", j, ms)[:].rearrange("p m c -> p (m c)"),
-                in0=kept[("gated_hn", j)][:, row_columns(ms)],
+                in0=kept[("gated_hn", j, ms)][:].rearrange("p m c -> p (m c)"),
                 in1=banks[("in", j)][:, row_columns(ms)],
                 op=ALU.add,
             )
@@ -381,16 +385,18 @@ def tile_prior_pa_kernel(
             rn_sum("in", j, GATE_N, (0,))
             if j < last:
                 rn_sum("r", j + 1, GATE_R, (0, 1))
-            gated_hn(j)
+            parts = (all_rows,) if j < last else (low_rows, high_rows)
+            for ms in parts:
+                gated_hn(j, ms)
             if j < last:
                 reset(j + 1)
-            for ms in (all_rows,) if j < last else (low_rows, high_rows):
+            for ms in parts:
                 pre_new(j, ms)
                 new(j, ms)
             if j < HALF_TILES:
                 for unit in second_units[2 * (j % 2) : 2 * (j % 2) + 2]:
-                    (share_new, share_hp)[j // 2](unit)
-            if j % 2 == 1 or j == last - 1:
+                    (share_hp, share_new)[j // 2](unit)
+            if j in FLIP_STEPS:
                 for done in range(flipped_tiles, j):
                     flip_back(done, all_rows)
                 for done in range(flipped_tiles, j):

@@ -84,15 +84,14 @@ def tile_prior_pa_kernel(
                     out=tile[r:P:32, :, :].bitcast(I32), in_=rows[r:16:4, :, first:last].bitcast(I32)
                 )
 
-        z_words = {}
+        z_words = []
 
         def load_z_words(w):
-            for g in range(K_GROUPS):
-                z_words[(w, g)] = keep.tile([P, 2 * R], U8, name="z_words%d%d" % (w, g), align_bytes=64)
-                nc.sync.dma_start(
-                    out=z_words[(w, g)][:].bitcast(I32),
-                    in_=words_dram[w][g][:, 2 * GATE_Z * R : 2 * (GATE_Z + 1) * R].bitcast(I32),
-                )
+            z_words.append(keep.tile([P, K_GROUPS, 2 * R], U8, name="z_words%d" % w, align_bytes=64))
+            nc.sync.dma_start(
+                out=z_words[w][:].bitcast(I32),
+                in_=words_dram[w].rearrange("g p b -> p g b")[:, :, 2 * GATE_Z * R : 2 * (GATE_Z + 1) * R].bitcast(I32),
+            )
 
         rn_words = {}
 
@@ -110,11 +109,11 @@ def tile_prior_pa_kernel(
                     .bitcast(I32),
                 )
 
-        load_x(0, (1, 1, 2))
-        load_scale_rows(z_planes[0], 0, GATE_Z * R, (GATE_Z + 1) * R)
         for first, vector in ((0, b_ih), (GATES * COL_TILES, b_n)):
             rows = vector.rearrange("(c p) -> c p", p=P)
             nc.scalar.dma_start(out=bias_rows[first : first + rows.shape[0], :], in_=rows)
+        load_x(0, (1, 1, 2))
+        load_scale_rows(z_planes[0], 0, GATE_Z * R, (GATE_Z + 1) * R)
         load_z_words(0)
         load_x(1, (2, 2))
         load_scale_rows(z_planes[1], 1, GATE_Z * R, (GATE_Z + 1) * R)
@@ -187,7 +186,7 @@ def tile_prior_pa_kernel(
                     out=z_banks[unit][:],
                     lhsT=x_codes[(w, g)][:, P * m : P * (m + 1)].bitcast(FP8X4),
                     lhsT_scale=x_planes[(w, g)][:, P * m : P * (m + 1)],
-                    rhs=z_words[(w, g)][:, 2 * HALF * half : 2 * HALF * (half + 1)].bitcast(FP4X4),
+                    rhs=z_words[w][:, g, 2 * HALF * half : 2 * HALF * (half + 1)].bitcast(FP4X4),
                     rhs_scale=z_planes[w][:, g, HALF * half : HALF * (half + 1)],
                     start=((w, g) == (0, 0)),
                     stop=((w, g) == (1, K_GROUPS - 1)),

from contextlib import ExitStack

import concourse.mybir as mybir
from concourse.masks import make_identity

F32 = mybir.dt.float32
BF16 = mybir.dt.bfloat16
I32 = mybir.dt.int32
U32 = mybir.dt.uint32
U8 = mybir.dt.uint8
FP8X4 = mybir.dt.float8_e4m3fn_x4
FP4X4 = mybir.dt.float4_e2m1fn_x4
ACT = mybir.ActivationFunctionType
ALU = mybir.AluOpType

P = 128
ROWS = 512
ROW_TILES = ROWS // P
K = 1024
K_PASS = 512
K_GROUPS = K // K_PASS
R = 1024
GATES = 3
GATE_R, GATE_Z, GATE_N = 0, 1, 2
COL_TILES = R // P
RN_RANGES = ((0, 2), (2, COL_TILES - 2))
FLIP_STEPS = (2, 5, 6, 7)
HALVES = 2
HALF = R // HALVES
HALF_TILES = HALF // P

FLOPS = 2 * 2 * ROWS * K * GATES * R


def tile_prior_pa_kernel(
    tc, h, prev_rnn_hidden, W_ih_words, W_ih_scales, W_hh_words, W_hh_scales, b_ih, b_n, out
):
    nc = tc.nc
    x_dram = (h, prev_rnn_hidden)
    words_dram = (W_ih_words, W_hh_words)
    scales_dram = (W_ih_scales, W_hh_scales)
    with ExitStack() as stack:
        keep = stack.enter_context(tc.tile_pool(name="keep", bufs=1))
        work = stack.enter_context(tc.tile_pool(name="work", bufs=5))
        psum = stack.enter_context(tc.psum_pool(name="psum", bufs=8))
        stack.enter_context(tc.manual_schedule())

        zero_col = keep.tile([P, 1], F32)
        nc.vector.memset(zero_col[:], 0.0)
        half_col = keep.tile([P, 1], F32)
        nc.scalar.activation(out=half_col[:], in_=zero_col[:], func=ACT.Sigmoid)
        z_planes = []
        planes = []
        for w in range(2):
            z_planes.append(keep.tile([P, K_GROUPS, R], U8, name="z_planes%d" % w, align_bytes=64))
            nc.vector.memset(z_planes[w][:].rearrange("p g n -> p (g n)").bitcast(I32), 0)
        bias_rows = keep.tile([P, P], BF16)
        nc.vector.memset(bias_rows[:], 0.0)
        for w in range(2):
            planes.append(keep.tile([P, K_GROUPS, GATES * R], U8, name="planes%d" % w, align_bytes=64))
        ident_f32 = keep.tile([P, P], F32)
        make_identity(nc, ident_f32[:])
        ident_bf16 = keep.tile([P, P], BF16)
        make_identity(nc, ident_bf16[:])
        for w in range(2):
            nc.gpsimd.memset(planes[w][:].rearrange("p g n -> p (g n)").bitcast(I32), 0)

        x_rows = ([], [])

        def load_x(x, pieces):
            first = 0
            for i, count in enumerate(pieces):
                tile = keep.tile([P, count, K], BF16, name="x_sb%d%d" % (x, i))
                nc.sync.dma_start(
                    out=tile[:], in_=x_dram[x].rearrange("(p m) k -> p m k", m=ROW_TILES)[:, first : first + count, :]
                )
                x_rows[x].extend([tile[:, m, :] for m in range(count)])
                first += count

        def load_scale_rows(tile, w, first, last):
            rows = scales_dram[w].rearrange("g q n -> q g n")
            for r in range(4):
                nc.sync.dma_start(
                    out=tile[r:P:32, :, :].bitcast(I32), in_=rows[r:16:4, :, first:last].bitcast(I32)
                )

        z_words = []

        def load_z_words(w):
            z_words.append(keep.tile([P, K_GROUPS, 2 * R], U8, name="z_words%d" % w, align_bytes=64))
            nc.sync.dma_start(
                out=z_words[w][:].bitcast(I32),
                in_=words_dram[w].rearrange("g p b -> p g b")[:, :, 2 * GATE_Z * R : 2 * (GATE_Z + 1) * R].bitcast(I32),
            )

        rn_words = {}

        def load_rn_words(w, part):
            first, count = RN_RANGES[part]
            tile = keep.tile([P, K_GROUPS, 2, 2 * P * count], U8, name="rn_words%d%d" % (w, part), align_bytes=64)
            rn_words[(w, part)] = tile
            for g in range(K_GROUPS):
                nc.sync.dma_start(
                    out=tile[:, g, :, :].bitcast(I32),
                    in_=words_dram[w][g]
                    .rearrange("p (gate b) -> p gate b", gate=GATES)[
                        :, GATE_R : GATES : GATE_N, 2 * P * first : 2 * P * (first + count)
                    ]
                    .bitcast(I32),
                )

        for first, vector in ((0, b_ih), (GATES * COL_TILES, b_n)):
            rows = vector.rearrange("(c p) -> c p", p=P)
            nc.scalar.dma_start(out=bias_rows[first : first + rows.shape[0], :], in_=rows)
        load_x(0, (1, 1, 2))
        load_scale_rows(z_planes[0], 0, GATE_Z * R, (GATE_Z + 1) * R)
        load_z_words(0)
        load_x(1, (2, 2))
        load_scale_rows(z_planes[1], 1, GATE_Z * R, (GATE_Z + 1) * R)
        load_z_words(1)
        for w in range(2):
            load_scale_rows(planes[w], w, 0, GATES * R)
            load_rn_words(w, 0)
        for w in range(2):
            load_rn_words(w, 1)

        half_rows = ROWS // 2
        half_tiles = ROW_TILES // 2
        grouped = {}
        x_codes = {}
        x_planes = {}
        for x in range(2):
            for g in range(K_GROUPS):
                grouped[(x, g)] = keep.tile([P, ROWS, 4], BF16, name="grouped%d%d" % (x, g), align_bytes=64)
                x_codes[(x, g)] = keep.tile([P, ROWS], U32, name="x_codes%d%d" % (x, g), align_bytes=64)
                x_planes[(x, g)] = keep.tile([P, ROWS], U8, name="x_planes%d%d" % (x, g), align_bytes=64)
        sorted_words = {}

        def sort_words(rows):
            sorted_words[rows] = keep.tile([P, half_tiles, 2, K // 4], F32, name="sorted%d" % rows)
            for mm in range(half_tiles):
                nc.vector.tensor_copy(
                    out=sorted_words[rows][:, mm, :, :],
                    in_=x_rows[1][half_tiles * rows + mm].bitcast(F32).rearrange("p (q u) -> p u q", u=2),
                )

        def words_of(x, rows, mm, g, u):
            if x == 1:
                return sorted_words[rows][:, mm, u, P * g : P * (g + 1)]
            return x_rows[0][half_tiles * rows + mm].bitcast(F32)[:, K_PASS // 2 * g + u : K_PASS // 2 * (g + 1) : 2]

        def flip_x(x, rows, copies):
            flipped = [psum.tile([P, 2, half_rows], F32, tag="bank", name="flipped") for g in range(K_GROUPS)]
            for mm in range(half_tiles):
                for g in range(K_GROUPS):
                    for u in range(2):
                        nc.tensor.transpose(
                            out=flipped[g][:, u, P * mm : P * (mm + 1)],
                            in_=words_of(x, rows, mm, g, u),
                            identity=ident_f32[:],
                        )
            for g in range(K_GROUPS):
                pairs = grouped[(x, g)][:].rearrange("p c t -> p (c t)").bitcast(F32).rearrange("p (c u) -> p c u", u=2)
                copies[g](
                    out=pairs[:, half_rows * rows : half_rows * (rows + 1), :],
                    in_=flipped[g][:].rearrange("p u c -> p c u"),
                )

        def quantise_x(x, rows):
            columns = slice(half_rows * rows, half_rows * (rows + 1))
            for g in range(K_GROUPS):
                nc.vector.quantize_mx(
                    out=x_codes[(x, g)][:, columns].bitcast(FP8X4),
                    scales=x_planes[(x, g)][:, columns],
                    in_=grouped[(x, g)][:, columns, :].rearrange("p c t -> p (c t)"),
                )

        z_banks = {}

        def z_passes(unit, sources):
            half, m = unit
            if unit not in z_banks:
                z_banks[unit] = psum.tile([P, HALF], F32, tag="bank", name="acc_z")
            for w, g in sources:
                nc.tensor.matmul_mx(
                    out=z_banks[unit][:],
                    lhsT=x_codes[(w, g)][:, P * m : P * (m + 1)].bitcast(FP8X4),
                    lhsT_scale=x_planes[(w, g)][:, P * m : P * (m + 1)],
                    rhs=z_words[w][:, g, 2 * HALF * half : 2 * HALF * (half + 1)].bitcast(FP4X4),
                    rhs_scale=z_planes[w][:, g, HALF * half : HALF * (half + 1)],
                    start=((w, g) == (0, 0)),
                    stop=((w, g) == (1, K_GROUPS - 1)),
                )

        z_bias = keep.tile([P, R], F32)
        new_share = []
        hp_share = []
        kept_hp = []
        for half in range(HALVES):
            new_share.append(keep.tile([P, ROW_TILES, HALF], F32, name="new_share%d" % half))
            hp_share.append(keep.tile([P, ROW_TILES, HALF], F32, name="hp_share%d" % half))
            kept_hp.append(keep.tile([P, ROW_TILES, HALF], F32, name="kept_hp%d" % half))
        z_sum = {}

        def z_add_bias(unit):
            half, m = unit
            z_sum[unit] = keep.tile([P, HALF], F32, name="z_sum%d%d" % unit)
            nc.vector.tensor_tensor(
                out=z_sum[unit][:], in0=z_banks[unit][:], in1=z_bias[:, HALF * half : HALF * (half + 1)], op=ALU.add
            )

        def share_new(unit):
            half, m = unit
            nc.scalar.activation(out=new_share[half][:, m, :], in_=z_sum[unit][:], func=ACT.Sigmoid, scale=-1.0)

        def share_hp(unit):
            half, m = unit
            nc.scalar.activation(out=hp_share[half][:, m, :], in_=z_sum[unit][:], func=ACT.Sigmoid)
            nc.gpsimd.tensor_tensor(
                out=kept_hp[half][:, m, :], in0=hp_share[half][:, m, :], in1=x_rows[1][m][:, HALF * half : HALF * (half + 1)], op=ALU.mult
            )

        on_vector = nc.vector.tensor_copy
        on_scalar = nc.scalar.copy
        flip_x(0, 0, (on_vector, on_scalar))
        quantise_x(0, 0)
        flip_x(0, 1, (on_scalar, on_vector))
        quantise_x(0, 1)
        bias_flipped = psum.tile([P, P], BF16, tag="bank")
        nc.tensor.transpose(out=bias_flipped[:], in_=bias_rows[:], identity=ident_bf16[:])
        spread = []
        for half in range(HALVES):
            spread.append(psum.tile([P, HALF_TILES, P], F32, tag="bank", name="spread"))
            for i in range(HALF_TILES):
                row = GATE_Z * COL_TILES + HALF_TILES * half + i
                nc.tensor.matmul(
                    spread[half][:, i, :],
                    lhsT=ident_bf16[:, row : row + 1].to_broadcast([P, P]),
                    rhs=bias_rows[:],
                    start=True,
                    stop=True,
                )
        on_h = [(0, g) for g in range(K_GROUPS)]
        on_hp = [(1, g) for g in range(K_GROUPS)]
        first_units = [(0, m) for m in range(ROW_TILES)]
        second_units = [(1, m) for m in range(ROW_TILES)]
        for units in (first_units[:2], first_units[2:]):
            for source in on_h:
                for unit in units:
                    z_passes(unit, [source])
        bias_cols = keep.tile([P, (GATES + 1) * COL_TILES], F32)
        nc.scalar.copy(out=bias_cols[:], in_=bias_flipped[:, 0 : (GATES + 1) * COL_TILES])
        for half in range(HALVES):
            nc.scalar.copy(out=z_bias[:, HALF * half : HALF * (half + 1)], in_=spread[half][:].rearrange("p i c -> p (i c)"))
        for rows in range(2):
            sort_words(rows)
        for rows in range(2):
            flip_x(1, rows, (on_vector, on_scalar))
            quantise_x(1, rows)
        waiting_units = second_units[:2]
        for unit in waiting_units:
            z_passes(unit, on_h)
        for unit in first_units + waiting_units:
            z_passes(unit, on_hp)
        for unit in second_units[2:]:
            z_passes(unit, on_h + on_hp)
        for unit in first_units + second_units:
            z_add_bias(unit)

        banks = {}
        kept = {}

        def rn_sum(name, j, gate, weights):
            bank = psum.tile([P, ROWS], F32, tag="bank", name="acc_" + name)
            banks[(name, j)] = bank
            part = 0 if j < RN_RANGES[1][0] else 1
            byte = 2 * P * (j - RN_RANGES[part][0])
            col = gate * R + j * P
            passes = [(w, g) for w in weights for g in range(K_GROUPS)]
            for w, g in passes:
                nc.tensor.matmul_mx(
                    out=bank[:],
                    lhsT=rn_words[(w, part)][:, g, gate // GATE_N, byte : byte + 2 * P].bitcast(FP4X4),
                    lhsT_scale=planes[w][:, g, col : col + P],
                    rhs=x_codes[(w, g)][:].bitcast(FP8X4),
                    rhs_scale=x_planes[(w, g)][:],
                    start=((w, g) == passes[0]),
                    stop=((w, g) == passes[-1]),
                )

        def bias_of(block, j):
            return bias_cols[:, block * COL_TILES + j : block * COL_TILES + j + 1]

        out_view = out.rearrange("(p m) n -> p m n", m=ROW_TILES)

        def f32_tile(name, j):
            kept[(name, j)] = work.tile([P, ROWS], F32, name=name, tag=name)
            return kept[(name, j)]

        def reset(j):
            nc.scalar.activation(
                out=f32_tile("reset", j)[:], in_=banks[("r", j)][:], func=ACT.Sigmoid, bias=bias_of(GATE_R, j)
            )

        def part_tile(name, j, ms):
            kept[(name, j, ms)] = work.tile([P, len(ms), P], F32, name=name, tag=name)
            return kept[(name, j, ms)]

        def row_columns(ms):
            return slice(P * ms.start, P * ms.stop)

        def row_tiles(ms):
            return slice(ms.start, ms.stop)

        def gated_hn(j, ms):
            nc.vector.scalar_tensor_tensor(
                out=part_tile("gated_hn", j, ms)[:].rearrange("p m c -> p (m c)"),
                in0=banks[("hn", j)][:, row_columns(ms)],
                scalar=bias_of(GATES, j),
                in1=kept[("reset", j)][:, row_columns(ms)],
                op0=ALU.add,
                op1=ALU.mult,
            )

        def pre_new(j, ms):
            nc.vector.tensor_tensor(
                out=part_tile("pre_new", j, ms)[:].rearrange("p m c -> p (m c)"),
                in0=kept[("gated_hn", j, ms)][:].rearrange("p m c -> p (m c)"),
                in1=banks[("in", j)][:, row_columns(ms)],
                op=ALU.add,
            )

        def new(j, ms):
            nc.scalar.activation(
                out=part_tile("new", j, ms)[:],
                in_=kept[("pre_new", j, ms)][:],
                func=ACT.Tanh,
                bias=bias_of(GATE_N, j),
            )

        def flip_back(j, ms):
            bank = psum.tile([P, len(ms), P], F32, tag="bank", name="back")
            banks[("back", j, ms)] = bank
            for i in range(len(ms)):
                nc.tensor.transpose(out=bank[:, i, :], in_=kept[("new", j, ms)][:, i, :], identity=ident_f32[:])

        def half_cols(j):
            return slice(P * (j % HALF_TILES), P * (j % HALF_TILES + 1))

        def z_tile(halves, j, ms):
            return halves[j // HALF_TILES][:, row_tiles(ms), half_cols(j)]

        def moved(j, ms):
            nc.vector.tensor_tensor(
                out=part_tile("moved", j, ms)[:],
                in0=banks[("back", j, ms)][:],
                in1=z_tile(new_share, j, ms),
                op=ALU.mult,
            )

        def blend(j, ms, engine):
            engine.tensor_tensor(
                out=part_tile("blend", j, ms)[:], in0=kept[("moved", j, ms)][:], in1=z_tile(kept_hp, j, ms), op=ALU.add
            )
            nc.sync.dma_start(
                out=out_view[:, row_tiles(ms), P * j : P * (j + 1)], in_=kept[("blend", j, ms)][:]
            )

        all_rows = range(ROW_TILES)
        low_rows = range(ROW_TILES // 2)
        high_rows = range(ROW_TILES // 2, ROW_TILES)
        last = COL_TILES - 1
        rn_sum("r", 0, GATE_R, (0, 1))
        for unit in first_units:
            share_new(unit)
        for unit in first_units[:2]:
            share_hp(unit)
        reset(0)
        for unit in first_units[2:]:
            share_hp(unit)
        flipped_tiles = 0
        for j in range(COL_TILES):
            rn_sum("hn", j, GATE_N, (1,))
            rn_sum("in", j, GATE_N, (0,))
            if j < last:
                rn_sum("r", j + 1, GATE_R, (0, 1))
            parts = (all_rows,) if j < last else (low_rows, high_rows)
            for ms in parts:
                gated_hn(j, ms)
            if j < last:
                reset(j + 1)
            for ms in parts:
                pre_new(j, ms)
                new(j, ms)
            if j < HALF_TILES:
                for unit in second_units[2 * (j % 2) : 2 * (j % 2) + 2]:
                    (share_hp, share_new)[j // 2](unit)
            if j in FLIP_STEPS:
                for done in range(flipped_tiles, j):
                    flip_back(done, all_rows)
                for done in range(flipped_tiles, j):
                    moved(done, all_rows)
                    blend(done, all_rows, nc.gpsimd)
                flipped_tiles = j
        for ms in (low_rows, high_rows):
            flip_back(last, ms)
        for ms in (low_rows, high_rows):
            moved(last, ms)
        for ms in (low_rows, high_rows):
            blend(last, ms, nc.vector)
